import numpy as np
import ml_dtypes

BF16 = ml_dtypes.bfloat16


def bf(x):
    return np.asarray(x, np.float32).astype(BF16)


def f32(x):
    return np.asarray(x, np.float32)


def f64(x):
    return np.asarray(x).astype(np.float64)


def striped(idx):
    return np.tile(idx.reshape(-1, 16).T, (8, 1))


C, C2, S, N, NH, HD, KN, RUN, NRUN = 512, 1024, 2048, 8192, 8, 64, 4, 1024, 8


def erf(a):
    b = np.clip(a, -6.0, 6.0)
    term = b.copy()
    tot = b.copy()
    for n in range(1, 150):
        term = term * (2.0 * b * b) / (2.0 * n + 1.0)
        tot = tot + term
    return np.where(np.abs(a) > 6.0, np.sign(a), 2.0 / np.sqrt(np.pi) * np.exp(-b * b) * tot)


def gelu(v):
    return 0.5 * v * (1.0 + erf(v / np.sqrt(2.0)))


def setup_inputs():
    rn = np.random.standard_normal
    return {
        "x": f32(rn((C, S))),
        "w0": bf(rn((C, C)) / np.sqrt(C)),
        "b0": f32(0.1 * rn((C, 1))),
        "qw": bf(1.5 * rn((C, C)) / np.sqrt(C)),
        "qb": f32(0.1 * rn((C, 1))),
        "wkv": bf(1.5 * rn((C, C2)) / np.sqrt(C)),
        "w1": bf(rn((C, C)) / np.sqrt(C)),
        "b1": f32(0.1 * rn((C, 1))),
        "offs": striped(np.concatenate([np.random.permutation(S)[:RUN] for _ in range(NRUN)])),
    }


def reference(x, w0, b0, qw, qb, wkv, w1, b1, offs):
    idx = offs[:16].T.reshape(-1)
    x1 = gelu(f64(w0).T @ f64(x) + f64(b0))
    q = f64(qw).T @ x1 + f64(qb)
    kv = f64(wkv).T @ x1
    lin = f64(w1).T @ x1 + f64(b1)
    e = kv[:C][:, idx] * np.tile(q, (1, KN))
    sc = e.reshape(NH, HD, N).sum(axis=1) / np.sqrt(HD)
    ex = np.exp(sc).reshape(NH, KN, S)
    p = (ex / ex.sum(axis=1, keepdims=True)).reshape(NH, N)
    u = kv[C:][:, idx] * np.repeat(p, HD, axis=0)
    return gelu(u.reshape(C, KN, S).sum(axis=1) + lin)

@@ -1,0 +1,219 @@
+from contextlib import ExitStack
+
+import concourse.mybir as mybir
+from concourse.masks import make_identity
+
+F32 = mybir.dt.float32
+BF16 = mybir.dt.bfloat16
+U16 = mybir.dt.uint16
+FUNC = mybir.ActivationFunctionType
+ALU = mybir.AluOpType
+AXIS = mybir.AxisListType
+
+P = 128
+C = 512
+S = 2048
+T = 4
+BLOCKS = C // P
+HEADS = 2
+HALF = P // HEADS
+BANK = 512
+CHUNKS = S // BANK
+NODE_BLOCKS = S // P
+LIST_COLS = S // 16
+ROUNDS = 2 * BLOCKS
+AHEAD = 2
+
+FLOPS = 2 * C * S * 5 * C + 2 * C * T * S
+
+
+def tile_attnno_b_kernel(tc, x, w0, b0, qw, qb, wkv, w1, b1, offs, out):
+    nc = tc.nc
+    with ExitStack() as ctx:
+        held = ctx.enter_context(tc.tile_pool(name="held", bufs=1))
+        arrivals = ctx.enter_context(tc.tile_pool(name="arrivals", bufs=CHUNKS))
+        staged = ctx.enter_context(tc.tile_pool(name="staged", bufs=2))
+        pairs = ctx.enter_context(tc.tile_pool(name="pairs", bufs=AHEAD + 1))
+        products = ctx.enter_context(tc.tile_pool(name="products", bufs=3))
+        rounded = ctx.enter_context(tc.tile_pool(name="rounded", bufs=2))
+        spread = ctx.enter_context(tc.tile_pool(name="spread", bufs=3))
+        sums = ctx.enter_context(tc.tile_pool(name="sums", bufs=2))
+        small = ctx.enter_context(tc.tile_pool(name="small", bufs=2))
+        banks = ctx.enter_context(tc.psum_pool(name="banks", bufs=4))
+        score_banks = ctx.enter_context(tc.psum_pool(name="score_banks", bufs=2))
+        flip_banks = ctx.enter_context(tc.psum_pool(name="flip_banks", bufs=1))
+
+        offsets = held.tile([P, T * LIST_COLS], U16, name="offsets")
+        nc.sync.dma_start(offsets[:], offs)
+
+        def load_weight(queue, w, name):
+            w_sb = held.tile([P, BLOCKS, w.shape[1]], BF16, name=name)
+            queue.dma_start(w_sb[:], w.rearrange("(k p) c -> p k c", p=P))
+            return w_sb
+
+        w0_sb = load_weight(nc.sync, w0, "w0_sb")
+
+        bias_rows = held.tile([P, P], F32, name="bias_rows")
+        nc.vector.memset(bias_rows[:], 0.0)
+        for i, vec in enumerate((b0, qb, b1)):
+            nc.scalar.dma_start(
+                bias_rows[i * BLOCKS : (i + 1) * BLOCKS, :], vec.rearrange("(k p) o -> k (p o)", p=P)
+            )
+        wkv_sb = load_weight(nc.scalar, wkv, "wkv_sb")
+        qw_sb = load_weight(nc.scalar, qw, "qw_sb")
+        w1_sb = load_weight(nc.scalar, w1, "w1_sb")
+
+        identity = held.tile([P, P], F32, name="identity")
+        make_identity(nc, identity[:])
+        bias_flipped = flip_banks.tile([P, P], F32, tag="flipped")
+        nc.tensor.transpose(bias_flipped[:], bias_rows[:], identity[:])
+        bias = held.tile([P, 3 * BLOCKS], F32, name="bias")
+        nc.vector.tensor_copy(bias[:], bias_flipped[:, 0 : 3 * BLOCKS])
+
+        head_sum = held.tile([P, HEADS], BF16, name="head_sum")
+        nc.vector.memset(head_sum[:], 0.0)
+        for h in range(HEADS):
+            nc.vector.memset(head_sum[h * HALF : (h + 1) * HALF, h : h + 1], 0.125)
+
+        x_blocks = x.rearrange("(k p) s -> p k s", p=P)
+        x1 = [held.tile([P, BLOCKS, BANK], BF16, name=f"x1_{n}") for n in range(CHUNKS)]
+        for n in range(CHUNKS):
+            x_f32 = arrivals.tile([P, BLOCKS, BANK], F32, name="x_f32")
+            nc.sync.dma_start(x_f32[:], x_blocks[:, :, n * BANK : (n + 1) * BANK])
+            x_bf = staged.tile([P, BLOCKS, BANK], BF16, name="x_bf")
+            nc.vector.tensor_copy(x_bf[:], x_f32[:])
+            for b in range(BLOCKS):
+                bank = banks.tile([P, BANK], F32, tag="bank")
+                for k in range(BLOCKS):
+                    nc.tensor.matmul(
+                        bank[:],
+                        w0_sb[:, k, b * P : (b + 1) * P],
+                        x_bf[:, k, :],
+                        start=(k == 0),
+                        stop=(k == BLOCKS - 1),
+                    )
+                nc.scalar.activation(x1[n][:, b, :], bank[:], FUNC.Gelu, bias=bias[:, b : b + 1])
+
+        def project_chunk(dst, w_sb, first_col, bias_col, n):
+            bank = banks.tile([P, BANK], F32, tag="bank")
+            for k in range(BLOCKS):
+                nc.tensor.matmul(
+                    bank[:],
+                    w_sb[:, k, first_col : first_col + P],
+                    x1[n][:, k, :],
+                    start=(k == 0),
+                    stop=(k == BLOCKS - 1),
+                )
+            if bias_col is None:
+                nc.scalar.copy(dst[:, n * BANK : (n + 1) * BANK], bank[:])
+            else:
+                nc.scalar.activation(dst[:, n * BANK : (n + 1) * BANK], bank[:], FUNC.Identity, bias=bias_col)
+
+        windows = {}
+        partners = {}
+
+        def project_pair_chunk(r, n):
+            b = r % BLOCKS
+            if n == 0:
+                windows[r] = pairs.tile([P, S], F32, name="window")
+                partners[r] = pairs.tile([P, S], F32, name="partner")
+            if r < BLOCKS:
+                project_chunk(windows[r], wkv_sb, b * P, None, n)
+                project_chunk(partners[r], qw_sb, b * P, bias[:, BLOCKS + b : BLOCKS + b + 1], n)
+            else:
+                project_chunk(windows[r], wkv_sb, C + b * P, None, n)
+                project_chunk(partners[r], w1_sb, b * P, bias[:, 2 * BLOCKS + b : 2 * BLOCKS + b + 1], n)
+
+        scores = {}
+
+        def key_piece(b, t):
+            if t == 0:
+                scores[b] = score_banks.tile([P, T * HEADS * NODE_BLOCKS], F32, name="scores")
+            e = products.tile([P, S], F32, name="product")
+            nc.vector.tensor_tensor(
+                e[:],
+                windows[b][:].indirect(offsets[:, t * LIST_COLS : (t + 1) * LIST_COLS]),
+                partners[b][:],
+                ALU.mult,
+            )
+            e_bf = rounded.tile([P, S], BF16, name="e_bf")
+            nc.scalar.copy(e_bf[:], e[:])
+            by_node_block = scores[b][:].rearrange("p (t h k) -> p t k h", t=T, h=HEADS)
+            for k in range(NODE_BLOCKS):
+                nc.tensor.matmul(
+                    by_node_block[:, t, k, :], e_bf[:, k * P : (k + 1) * P], head_sum[:], start=True, stop=True
+                )
+
+        numerators = {}
+
+        def softmax_shift(b):
+            by_t = scores[b][:].rearrange("p (t m) -> p t m", t=T)
+            top = small.tile([P, HEADS * NODE_BLOCKS], F32, name="top")
+            nc.vector.tensor_reduce(top[:], scores[b][:].rearrange("p (t m) -> p m t", t=T), AXIS.X, ALU.max)
+            shifted = small.tile([P, T, HEADS * NODE_BLOCKS], F32, name="shifted")
+            nc.vector.tensor_tensor(
+                shifted[:], by_t, top[:].unsqueeze(1).to_broadcast([P, T, HEADS * NODE_BLOCKS]), ALU.subtract
+            )
+            numerators[b] = small.tile([P, T, HEADS * NODE_BLOCKS], F32, name="numerator")
+            nc.scalar.activation(numerators[b][:], shifted[:], FUNC.Exp)
+
+        def softmax_normalise(b):
+            total = small.tile([P, HEADS * NODE_BLOCKS], F32, name="total")
+            nc.vector.tensor_reduce(total[:], numerators[b][:].rearrange("p t m -> p m t"), AXIS.X, ALU.add)
+            inverse = small.tile([P, HEADS * NODE_BLOCKS], F32, name="inverse")
+            nc.vector.reciprocal(inverse[:], total[:])
+            p_by_node = small.tile([P, T, HEADS * NODE_BLOCKS], F32, name="p_by_node")
+            nc.vector.tensor_tensor(
+                p_by_node[:],
+                numerators[b][:],
+                inverse[:].unsqueeze(1).to_broadcast([P, T, HEADS * NODE_BLOCKS]),
+                ALU.mult,
+            )
+            p_flipped = flip_banks.tile([P, P], F32, tag="flipped")
+            nc.tensor.transpose(p_flipped[:], p_by_node[:].rearrange("p t m -> p (t m)"), identity[:])
+            p_rows = small.tile([P, P], F32, name="p_rows")
+            nc.scalar.copy(p_rows[:], p_flipped[:])
+            nc.scalar.dma_start(
+                out[b * P : b * P + T * HEADS, :].rearrange("r (k s) -> (r k) s", s=P), p_rows[:]
+            )
+
+        totals = {}
+
+        def value_piece(b, t):
+            r = BLOCKS + b
+            p_spread = spread.tile([P, S], F32, name="p_spread")
+            for h in range(HEADS):
+                nc.sync.dma_start(
+                    p_spread[h * HALF : (h + 1) * HALF, :], out[b * P + t * HEADS + h, :].partition_broadcast(HALF)
+                )
+            u = products.tile([P, S], F32, name="product")
+            nc.vector.tensor_tensor(
+                u[:],
+                windows[r][:].indirect(offsets[:, t * LIST_COLS : (t + 1) * LIST_COLS]),
+                p_spread[:],
+                ALU.mult,
+            )
+            if t == 0:
+                totals[b] = sums.tile([P, S], F32, name="total_u")
+                nc.gpsimd.tensor_tensor(totals[b][:], partners[r][:], u[:], ALU.add)
+            else:
+                nc.gpsimd.tensor_tensor(totals[b][:], totals[b][:], u[:], ALU.add)
+            if t == T - 1:
+                nc.scalar.activation(totals[b][:], totals[b][:], FUNC.Gelu)
+                nc.scalar.dma_start(out[b * P : (b + 1) * P, :], totals[b][:])
+
+        for r in range(AHEAD):
+            for n in range(CHUNKS):
+                project_pair_chunk(r, n)
+        for r in range(ROUNDS):
+            for t in range(T):
+                if r + AHEAD < ROUNDS:
+                    project_pair_chunk(r + AHEAD, t)
+                if r < BLOCKS:
+                    key_piece(r, t)
+                else:
+                    value_piece(r - BLOCKS, t)
+                if 1 <= r <= BLOCKS and t == 0:
+                    softmax_shift(r - 1)
+                if 1 <= r <= BLOCKS and t == 1:
+                    softmax_normalise(r - 1)

@@ -21,10 +21,9 @@ BANK = 512
 CHUNKS = S // BANK
 NODE_BLOCKS = S // P
 LIST_COLS = S // 16
-ROUNDS = 2 * BLOCKS
-AHEAD = 2
 
 FLOPS = 2 * C * S * 5 * C + 2 * C * T * S
+PER_PIECE = 3
 
 
 def tile_attnno_b_kernel(tc, x, w0, b0, qw, qb, wkv, w1, b1, offs, out):
@@ -33,18 +32,16 @@ def tile_attnno_b_kernel(tc, x, w0, b0, qw, qb, wkv, w1, b1, offs, out):
         held = ctx.enter_context(tc.tile_pool(name="held", bufs=1))
         arrivals = ctx.enter_context(tc.tile_pool(name="arrivals", bufs=CHUNKS))
         staged = ctx.enter_context(tc.tile_pool(name="staged", bufs=2))
-        pairs = ctx.enter_context(tc.tile_pool(name="pairs", bufs=AHEAD + 1))
+        windows = ctx.enter_context(tc.tile_pool(name="windows", bufs=5))
+        queries = ctx.enter_context(tc.tile_pool(name="queries", bufs=3))
         products = ctx.enter_context(tc.tile_pool(name="products", bufs=3))
         rounded = ctx.enter_context(tc.tile_pool(name="rounded", bufs=2))
         spread = ctx.enter_context(tc.tile_pool(name="spread", bufs=3))
-        sums = ctx.enter_context(tc.tile_pool(name="sums", bufs=2))
+        results = ctx.enter_context(tc.tile_pool(name="results", bufs=4))
         small = ctx.enter_context(tc.tile_pool(name="small", bufs=2))
-        banks = ctx.enter_context(tc.psum_pool(name="banks", bufs=4))
+        banks = ctx.enter_context(tc.psum_pool(name="banks", bufs=5))
         score_banks = ctx.enter_context(tc.psum_pool(name="score_banks", bufs=2))
         flip_banks = ctx.enter_context(tc.psum_pool(name="flip_banks", bufs=1))
-
-        offsets = held.tile([P, T * LIST_COLS], U16, name="offsets")
-        nc.sync.dma_start(offsets[:], offs)
 
         def load_weight(queue, w, name):
             w_sb = held.tile([P, BLOCKS, w.shape[1]], BF16, name=name)
@@ -81,7 +78,8 @@ def tile_attnno_b_kernel(tc, x, w0, b0, qw, qb, wkv, w1, b1, offs, out):
             x_f32 = arrivals.tile([P, BLOCKS, BANK], F32, name="x_f32")
             nc.sync.dma_start(x_f32[:], x_blocks[:, :, n * BANK : (n + 1) * BANK])
             x_bf = staged.tile([P, BLOCKS, BANK], BF16, name="x_bf")
-            nc.vector.tensor_copy(x_bf[:], x_f32[:])
+            for k in range(BLOCKS):
+                nc.vector.tensor_copy(x_bf[:, k, :], x_f32[:, k, :])
             for b in range(BLOCKS):
                 bank = banks.tile([P, BANK], F32, tag="bank")
                 for k in range(BLOCKS):
@@ -94,35 +92,37 @@ def tile_attnno_b_kernel(tc, x, w0, b0, qw, qb, wkv, w1, b1, offs, out):
                     )
                 nc.scalar.activation(x1[n][:, b, :], bank[:], FUNC.Gelu, bias=bias[:, b : b + 1])
 
-        def project_chunk(dst, w_sb, first_col, bias_col, n):
-            bank = banks.tile([P, BANK], F32, tag="bank")
+        offsets = held.tile([P, T * LIST_COLS], U16, name="offsets")
+        nc.sync.dma_start(offsets[:], offs)
+
+        def project_into_bank(bank, w_sb, first_col, n, stop):
             for k in range(BLOCKS):
                 nc.tensor.matmul(
                     bank[:],
                     w_sb[:, k, first_col : first_col + P],
                     x1[n][:, k, :],
                     start=(k == 0),
-                    stop=(k == BLOCKS - 1),
+                    stop=(stop and k == BLOCKS - 1),
                 )
-            if bias_col is None:
-                nc.scalar.copy(dst[:, n * BANK : (n + 1) * BANK], bank[:])
-            else:
-                nc.scalar.activation(dst[:, n * BANK : (n + 1) * BANK], bank[:], FUNC.Identity, bias=bias_col)
 
-        windows = {}
-        partners = {}
+        projected = {}
 
-        def project_pair_chunk(r, n):
-            b = r % BLOCKS
-            if n == 0:
-                windows[r] = pairs.tile([P, S], F32, name="window")
-                partners[r] = pairs.tile([P, S], F32, name="partner")
-            if r < BLOCKS:
-                project_chunk(windows[r], wkv_sb, b * P, None, n)
-                project_chunk(partners[r], qw_sb, b * P, bias[:, BLOCKS + b : BLOCKS + b + 1], n)
+        def project_chunk(kind, b, n):
+            if n == 0 and kind == "queries":
+                projected[kind, b] = queries.tile([P, S], F32, name="q")
+            elif n == 0:
+                projected[kind, b] = windows.tile([P, S], F32, name="window")
+            chunk = projected[kind, b][:, n * BANK : (n + 1) * BANK]
+            bank = banks.tile([P, BANK], F32, tag="bank")
+            if kind == "keys":
+                project_into_bank(bank, wkv_sb, b * P, n, True)
+                nc.scalar.copy(chunk, bank[:])
+            elif kind == "values":
+                project_into_bank(bank, wkv_sb, C + b * P, n, True)
+                nc.scalar.copy(chunk, bank[:])
             else:
-                project_chunk(windows[r], wkv_sb, C + b * P, None, n)
-                project_chunk(partners[r], w1_sb, b * P, bias[:, 2 * BLOCKS + b : 2 * BLOCKS + b + 1], n)
+                project_into_bank(bank, qw_sb, b * P, n, True)
+                nc.scalar.activation(chunk, bank[:], FUNC.Identity, bias=bias[:, BLOCKS + b : BLOCKS + b + 1])
 
         scores = {}
 
@@ -132,8 +132,8 @@ def tile_attnno_b_kernel(tc, x, w0, b0, qw, qb, wkv, w1, b1, offs, out):
             e = products.tile([P, S], F32, name="product")
             nc.vector.tensor_tensor(
                 e[:],
-                windows[b][:].indirect(offsets[:, t * LIST_COLS : (t + 1) * LIST_COLS]),
-                partners[b][:],
+                projected["keys", b][:].indirect(offsets[:, t * LIST_COLS : (t + 1) * LIST_COLS]),
+                projected["queries", b][:],
                 ALU.mult,
             )
             e_bf = rounded.tile([P, S], BF16, name="e_bf")
@@ -147,12 +147,14 @@ def tile_attnno_b_kernel(tc, x, w0, b0, qw, qb, wkv, w1, b1, offs, out):
         numerators = {}
 
         def softmax_shift(b):
-            by_t = scores[b][:].rearrange("p (t m) -> p t m", t=T)
             top = small.tile([P, HEADS * NODE_BLOCKS], F32, name="top")
             nc.vector.tensor_reduce(top[:], scores[b][:].rearrange("p (t m) -> p m t", t=T), AXIS.X, ALU.max)
             shifted = small.tile([P, T, HEADS * NODE_BLOCKS], F32, name="shifted")
             nc.vector.tensor_tensor(
-                shifted[:], by_t, top[:].unsqueeze(1).to_broadcast([P, T, HEADS * NODE_BLOCKS]), ALU.subtract
+                shifted[:],
+                scores[b][:].rearrange("p (t m) -> p t m", t=T),
+                top[:].unsqueeze(1).to_broadcast([P, T, HEADS * NODE_BLOCKS]),
+                ALU.subtract,
             )
             numerators[b] = small.tile([P, T, HEADS * NODE_BLOCKS], F32, name="numerator")
             nc.scalar.activation(numerators[b][:], shifted[:], FUNC.Exp)
@@ -180,7 +182,10 @@ def tile_attnno_b_kernel(tc, x, w0, b0, qw, qb, wkv, w1, b1, offs, out):
         totals = {}
 
         def value_piece(b, t):
-            r = BLOCKS + b
+            if t == 0:
+                totals[b] = [banks.tile([P, BANK], F32, tag="bank", name="total_bank") for n in range(CHUNKS)]
+                for n in range(CHUNKS):
+                    project_into_bank(totals[b][n], w1_sb, b * P, n, False)
             p_spread = spread.tile([P, S], F32, name="p_spread")
             for h in range(HEADS):
                 nc.sync.dma_start(
@@ -189,31 +194,44 @@ def tile_attnno_b_kernel(tc, x, w0, b0, qw, qb, wkv, w1, b1, offs, out):
             u = products.tile([P, S], F32, name="product")
             nc.vector.tensor_tensor(
                 u[:],
-                windows[r][:].indirect(offsets[:, t * LIST_COLS : (t + 1) * LIST_COLS]),
+                projected["values", b][:].indirect(offsets[:, t * LIST_COLS : (t + 1) * LIST_COLS]),
                 p_spread[:],
                 ALU.mult,
             )
-            if t == 0:
-                totals[b] = sums.tile([P, S], F32, name="total_u")
-                nc.gpsimd.tensor_tensor(totals[b][:], partners[r][:], u[:], ALU.add)
-            else:
-                nc.gpsimd.tensor_tensor(totals[b][:], totals[b][:], u[:], ALU.add)
-            if t == T - 1:
-                nc.scalar.activation(totals[b][:], totals[b][:], FUNC.Gelu)
-                nc.scalar.dma_start(out[b * P : (b + 1) * P, :], totals[b][:])
-
-        for r in range(AHEAD):
             for n in range(CHUNKS):
-                project_pair_chunk(r, n)
-        for r in range(ROUNDS):
+                nc.tensor.matmul(
+                    totals[b][n][:], identity[:], u[:, n * BANK : (n + 1) * BANK], start=False, stop=(t == T - 1)
+                )
+                if t == T - 1:
+                    result = results.tile([P, BANK], F32, name="result")
+                    nc.scalar.activation(
+                        result[:], totals[b][n][:], FUNC.Gelu, bias=bias[:, 2 * BLOCKS + b : 2 * BLOCKS + b + 1]
+                    )
+                    nc.scalar.dma_start(out[b * P : (b + 1) * P, n * BANK : (n + 1) * BANK], result[:])
+
+        rounds = [("keys", b) for b in range(BLOCKS)] + [("values", b) for b in range(BLOCKS)]
+
+        chunks_to_project = []
+        for kind, b in rounds:
+            for tile_kind in ("keys", "queries") if kind == "keys" else ("values",):
+                for n in range(CHUNKS):
+                    chunks_to_project.append((tile_kind, b, n))
+
+        first = 2 * CHUNKS
+        for kind, b, n in chunks_to_project[:first]:
+            project_chunk(kind, b, n)
+        key_pieces_done = 0
+        for i, (kind, b) in enumerate(rounds):
             for t in range(T):
-                if r + AHEAD < ROUNDS:
-                    project_pair_chunk(r + AHEAD, t)
-                if r < BLOCKS:
-                    key_piece(r, t)
+                if kind == "keys":
+                    start = first + PER_PIECE * key_pieces_done
+                    for tile_kind, tile_b, n in chunks_to_project[start : start + PER_PIECE]:
+                        project_chunk(tile_kind, tile_b, n)
+                    key_piece(b, t)
+                    key_pieces_done += 1
                 else:
-                    value_piece(r - BLOCKS, t)
-                if 1 <= r <= BLOCKS and t == 0:
-                    softmax_shift(r - 1)
-                if 1 <= r <= BLOCKS and t == 1:
-                    softmax_normalise(r - 1)
+                    value_piece(b, t)
+                if i > 0 and rounds[i - 1][0] == "keys" and t == 0:
+                    softmax_shift(rounds[i - 1][1])
+                if i > 0 and rounds[i - 1][0] == "keys" and t == 1:
+                    softmax_normalise(rounds[i - 1][1])

@@ -180,6 +180,7 @@ def tile_attnno_b_kernel(tc, x, w0, b0, qw, qb, wkv, w1, b1, offs, out):
             )
 
         totals = {}
+        earlier_u = {}
 
         def value_piece(b, t):
             if t == 0:
@@ -198,6 +199,11 @@ def tile_attnno_b_kernel(tc, x, w0, b0, qw, qb, wkv, w1, b1, offs, out):
                 p_spread[:],
                 ALU.mult,
             )
+            if t == 0:
+                earlier_u[b] = u
+                return
+            if t == 1:
+                nc.vector.tensor_tensor(u[:], earlier_u[b][:], u[:], ALU.add)
             for n in range(CHUNKS):
                 nc.tensor.matmul(
                     totals[b][n][:], identity[:], u[:, n * BANK : (n + 1) * BANK], start=False, stop=(t == T - 1)
@@ -231,7 +237,7 @@ def tile_attnno_b_kernel(tc, x, w0, b0, qw, qb, wkv, w1, b1, offs, out):
                     key_pieces_done += 1
                 else:
                     value_piece(b, t)
-                if i > 0 and rounds[i - 1][0] == "keys" and t == 0:
-                    softmax_shift(rounds[i - 1][1])
                 if i > 0 and rounds[i - 1][0] == "keys" and t == 1:
+                    softmax_shift(rounds[i - 1][1])
+                if i > 0 and rounds[i - 1][0] == "keys" and t == 3:
                     softmax_normalise(rounds[i - 1][1])

@@ -36,7 +36,7 @@ def tile_attnno_b_kernel(tc, x, w0, b0, qw, qb, wkv, w1, b1, offs, out):
         queries = ctx.enter_context(tc.tile_pool(name="queries", bufs=3))
         products = ctx.enter_context(tc.tile_pool(name="products", bufs=3))
         rounded = ctx.enter_context(tc.tile_pool(name="rounded", bufs=2))
-        spread = ctx.enter_context(tc.tile_pool(name="spread", bufs=3))
+        spread = ctx.enter_context(tc.tile_pool(name="spread", bufs=6))
         results = ctx.enter_context(tc.tile_pool(name="results", bufs=4))
         small = ctx.enter_context(tc.tile_pool(name="small", bufs=2))
         banks = ctx.enter_context(tc.psum_pool(name="banks", bufs=5))
@@ -180,7 +180,6 @@ def tile_attnno_b_kernel(tc, x, w0, b0, qw, qb, wkv, w1, b1, offs, out):
             )
 
         totals = {}
-        earlier_u = {}
 
         def value_piece(b, t):
             if t == 0:
@@ -199,11 +198,6 @@ def tile_attnno_b_kernel(tc, x, w0, b0, qw, qb, wkv, w1, b1, offs, out):
                 p_spread[:],
                 ALU.mult,
             )
-            if t == 0:
-                earlier_u[b] = u
-                return
-            if t == 1:
-                nc.vector.tensor_tensor(u[:], earlier_u[b][:], u[:], ALU.add)
             for n in range(CHUNKS):
                 nc.tensor.matmul(
                     totals[b][n][:], identity[:], u[:, n * BANK : (n + 1) * BANK], start=False, stop=(t == T - 1)

@@ -23,6 +23,7 @@ NODE_BLOCKS = S // P
 LIST_COLS = S // 16
 
 FLOPS = 2 * C * S * 5 * C + 2 * C * T * S
+PRE_ADDED = 2
 PER_PIECE = 3
 
 
@@ -30,13 +31,12 @@ def tile_attnno_b_kernel(tc, x, w0, b0, qw, qb, wkv, w1, b1, offs, out):
     nc = tc.nc
     with ExitStack() as ctx:
         held = ctx.enter_context(tc.tile_pool(name="held", bufs=1))
-        arrivals = ctx.enter_context(tc.tile_pool(name="arrivals", bufs=CHUNKS))
+        streamed = ctx.enter_context(tc.tile_pool(name="streamed", bufs=10))
         staged = ctx.enter_context(tc.tile_pool(name="staged", bufs=2))
         windows = ctx.enter_context(tc.tile_pool(name="windows", bufs=5))
         queries = ctx.enter_context(tc.tile_pool(name="queries", bufs=3))
         products = ctx.enter_context(tc.tile_pool(name="products", bufs=3))
         rounded = ctx.enter_context(tc.tile_pool(name="rounded", bufs=2))
-        spread = ctx.enter_context(tc.tile_pool(name="spread", bufs=6))
         results = ctx.enter_context(tc.tile_pool(name="results", bufs=4))
         small = ctx.enter_context(tc.tile_pool(name="small", bufs=2))
         banks = ctx.enter_context(tc.psum_pool(name="banks", bufs=5))
@@ -75,7 +75,7 @@ def tile_attnno_b_kernel(tc, x, w0, b0, qw, qb, wkv, w1, b1, offs, out):
         x_blocks = x.rearrange("(k p) s -> p k s", p=P)
         x1 = [held.tile([P, BLOCKS, BANK], BF16, name=f"x1_{n}") for n in range(CHUNKS)]
         for n in range(CHUNKS):
-            x_f32 = arrivals.tile([P, BLOCKS, BANK], F32, name="x_f32")
+            x_f32 = streamed.tile([P, BLOCKS, BANK], F32, name="x_f32", tag="streamed")
             nc.sync.dma_start(x_f32[:], x_blocks[:, :, n * BANK : (n + 1) * BANK])
             x_bf = staged.tile([P, BLOCKS, BANK], BF16, name="x_bf")
             for k in range(BLOCKS):
@@ -180,13 +180,14 @@ def tile_attnno_b_kernel(tc, x, w0, b0, qw, qb, wkv, w1, b1, offs, out):
             )
 
         totals = {}
+        earlier_u = {}
 
         def value_piece(b, t):
             if t == 0:
                 totals[b] = [banks.tile([P, BANK], F32, tag="bank", name="total_bank") for n in range(CHUNKS)]
                 for n in range(CHUNKS):
                     project_into_bank(totals[b][n], w1_sb, b * P, n, False)
-            p_spread = spread.tile([P, S], F32, name="p_spread")
+            p_spread = streamed.tile([P, S], F32, name="p_spread", tag="streamed")
             for h in range(HEADS):
                 nc.sync.dma_start(
                     p_spread[h * HALF : (h + 1) * HALF, :], out[b * P + t * HEADS + h, :].partition_broadcast(HALF)
@@ -198,7 +199,12 @@ def tile_attnno_b_kernel(tc, x, w0, b0, qw, qb, wkv, w1, b1, offs, out):
                 p_spread[:],
                 ALU.mult,
             )
-            for n in range(CHUNKS):
+            if t == 0:
+                earlier_u[b] = u
+            if t == 1:
+                shared = slice(0, PRE_ADDED * BANK)
+                nc.vector.tensor_tensor(u[:, shared], earlier_u[b][:, shared], u[:, shared], ALU.add)
+            for n in range(PRE_ADDED if t == 0 else 0, CHUNKS):
                 nc.tensor.matmul(
                     totals[b][n][:], identity[:], u[:, n * BANK : (n + 1) * BANK], start=False, stop=(t == T - 1)
                 )

@@ -23,7 +23,6 @@ NODE_BLOCKS = S // P
 LIST_COLS = S // 16
 
 FLOPS = 2 * C * S * 5 * C + 2 * C * T * S
-PRE_ADDED = 2
 PER_PIECE = 3
 
 
@@ -180,7 +179,6 @@ def tile_attnno_b_kernel(tc, x, w0, b0, qw, qb, wkv, w1, b1, offs, out):
             )
 
         totals = {}
-        earlier_u = {}
 
         def value_piece(b, t):
             if t == 0:
@@ -199,12 +197,7 @@ def tile_attnno_b_kernel(tc, x, w0, b0, qw, qb, wkv, w1, b1, offs, out):
                 p_spread[:],
                 ALU.mult,
             )
-            if t == 0:
-                earlier_u[b] = u
-            if t == 1:
-                shared = slice(0, PRE_ADDED * BANK)
-                nc.vector.tensor_tensor(u[:, shared], earlier_u[b][:, shared], u[:, shared], ALU.add)
-            for n in range(PRE_ADDED if t == 0 else 0, CHUNKS):
+            for n in range(CHUNKS):
                 nc.tensor.matmul(
                     totals[b][n][:], identity[:], u[:, n * BANK : (n + 1) * BANK], start=False, stop=(t == T - 1)
                 )

@@ -20,25 +20,30 @@ HALF = P // HEADS
 BANK = 512
 CHUNKS = S // BANK
 NODE_BLOCKS = S // P
+GROUPS = HEADS * NODE_BLOCKS
 LIST_COLS = S // 16
+B0, QB, B1 = 0, 1, 2
+
+PER_PIECE = 3
+PRE_ADDED = 2
+STREAMED = 10
 
 FLOPS = 2 * C * S * 5 * C + 2 * C * T * S
-PER_PIECE = 3
 
 
 def tile_attnno_b_kernel(tc, x, w0, b0, qw, qb, wkv, w1, b1, offs, out):
     nc = tc.nc
     with ExitStack() as ctx:
         held = ctx.enter_context(tc.tile_pool(name="held", bufs=1))
-        streamed = ctx.enter_context(tc.tile_pool(name="streamed", bufs=10))
+        streamed = ctx.enter_context(tc.tile_pool(name="streamed", bufs=STREAMED))
         staged = ctx.enter_context(tc.tile_pool(name="staged", bufs=2))
-        windows = ctx.enter_context(tc.tile_pool(name="windows", bufs=5))
+        windows = ctx.enter_context(tc.tile_pool(name="windows", bufs=BLOCKS + 1))
         queries = ctx.enter_context(tc.tile_pool(name="queries", bufs=3))
         products = ctx.enter_context(tc.tile_pool(name="products", bufs=3))
         rounded = ctx.enter_context(tc.tile_pool(name="rounded", bufs=2))
-        results = ctx.enter_context(tc.tile_pool(name="results", bufs=4))
+        results = ctx.enter_context(tc.tile_pool(name="results", bufs=CHUNKS))
         small = ctx.enter_context(tc.tile_pool(name="small", bufs=2))
-        banks = ctx.enter_context(tc.psum_pool(name="banks", bufs=5))
+        banks = ctx.enter_context(tc.psum_pool(name="banks", bufs=CHUNKS + 1))
         score_banks = ctx.enter_context(tc.psum_pool(name="score_banks", bufs=2))
         flip_banks = ctx.enter_context(tc.psum_pool(name="flip_banks", bufs=1))
 
@@ -51,9 +56,9 @@ def tile_attnno_b_kernel(tc, x, w0, b0, qw, qb, wkv, w1, b1, offs, out):
 
         bias_rows = held.tile([P, P], F32, name="bias_rows")
         nc.vector.memset(bias_rows[:], 0.0)
-        for i, vec in enumerate((b0, qb, b1)):
+        for which, vec in enumerate((b0, qb, b1)):
             nc.scalar.dma_start(
-                bias_rows[i * BLOCKS : (i + 1) * BLOCKS, :], vec.rearrange("(k p) o -> k (p o)", p=P)
+                bias_rows[which * BLOCKS : (which + 1) * BLOCKS, :], vec.rearrange("(b p) o -> b (p o)", p=P)
             )
         wkv_sb = load_weight(nc.scalar, wkv, "wkv_sb")
         qw_sb = load_weight(nc.scalar, qw, "qw_sb")
@@ -65,6 +70,9 @@ def tile_attnno_b_kernel(tc, x, w0, b0, qw, qb, wkv, w1, b1, offs, out):
         nc.tensor.transpose(bias_flipped[:], bias_rows[:], identity[:])
         bias = held.tile([P, 3 * BLOCKS], F32, name="bias")
         nc.vector.tensor_copy(bias[:], bias_flipped[:, 0 : 3 * BLOCKS])
+
+        def bias_of(which, b):
+            return bias[:, which * BLOCKS + b : which * BLOCKS + b + 1]
 
         head_sum = held.tile([P, HEADS], BF16, name="head_sum")
         nc.vector.memset(head_sum[:], 0.0)
@@ -89,7 +97,7 @@ def tile_attnno_b_kernel(tc, x, w0, b0, qw, qb, wkv, w1, b1, offs, out):
                         start=(k == 0),
                         stop=(k == BLOCKS - 1),
                     )
-                nc.scalar.activation(x1[n][:, b, :], bank[:], FUNC.Gelu, bias=bias[:, b : b + 1])
+                nc.scalar.activation(x1[n][:, b, :], bank[:], FUNC.Gelu, bias=bias_of(B0, b))
 
         offsets = held.tile([P, T * LIST_COLS], U16, name="offsets")
         nc.sync.dma_start(offsets[:], offs)
@@ -121,116 +129,105 @@ def tile_attnno_b_kernel(tc, x, w0, b0, qw, qb, wkv, w1, b1, offs, out):
                 nc.scalar.copy(chunk, bank[:])
             else:
                 project_into_bank(bank, qw_sb, b * P, n, True)
-                nc.scalar.activation(chunk, bank[:], FUNC.Identity, bias=bias[:, BLOCKS + b : BLOCKS + b + 1])
+                nc.scalar.activation(chunk, bank[:], FUNC.Identity, bias=bias_of(QB, b))
+
+        def list_of(t):
+            return offsets[:, t * LIST_COLS : (t + 1) * LIST_COLS]
 
         scores = {}
 
         def key_piece(b, t):
             if t == 0:
-                scores[b] = score_banks.tile([P, T * HEADS * NODE_BLOCKS], F32, name="scores")
+                scores[b] = score_banks.tile([P, T * GROUPS], F32, name="scores")
             e = products.tile([P, S], F32, name="product")
             nc.vector.tensor_tensor(
-                e[:],
-                projected["keys", b][:].indirect(offsets[:, t * LIST_COLS : (t + 1) * LIST_COLS]),
-                projected["queries", b][:],
-                ALU.mult,
+                e[:], projected["keys", b][:].indirect(list_of(t)), projected["queries", b][:], ALU.mult
             )
             e_bf = rounded.tile([P, S], BF16, name="e_bf")
             nc.scalar.copy(e_bf[:], e[:])
-            by_node_block = scores[b][:].rearrange("p (t h k) -> p t k h", t=T, h=HEADS)
-            for k in range(NODE_BLOCKS):
+            by_node_block = scores[b][:].rearrange("p (t h g) -> p t g h", t=T, h=HEADS)
+            for g in range(NODE_BLOCKS):
                 nc.tensor.matmul(
-                    by_node_block[:, t, k, :], e_bf[:, k * P : (k + 1) * P], head_sum[:], start=True, stop=True
+                    by_node_block[:, t, g, :], e_bf[:, g * P : (g + 1) * P], head_sum[:], start=True, stop=True
                 )
 
         numerators = {}
 
         def softmax_shift(b):
-            top = small.tile([P, HEADS * NODE_BLOCKS], F32, name="top")
+            top = small.tile([P, GROUPS], F32, name="top")
             nc.vector.tensor_reduce(top[:], scores[b][:].rearrange("p (t m) -> p m t", t=T), AXIS.X, ALU.max)
-            shifted = small.tile([P, T, HEADS * NODE_BLOCKS], F32, name="shifted")
+            shifted = small.tile([P, T, GROUPS], F32, name="shifted")
             nc.vector.tensor_tensor(
                 shifted[:],
                 scores[b][:].rearrange("p (t m) -> p t m", t=T),
-                top[:].unsqueeze(1).to_broadcast([P, T, HEADS * NODE_BLOCKS]),
+                top[:].unsqueeze(1).to_broadcast([P, T, GROUPS]),
                 ALU.subtract,
             )
-            numerators[b] = small.tile([P, T, HEADS * NODE_BLOCKS], F32, name="numerator")
+            numerators[b] = small.tile([P, T, GROUPS], F32, name="numerator")
             nc.scalar.activation(numerators[b][:], shifted[:], FUNC.Exp)
 
         def softmax_normalise(b):
-            total = small.tile([P, HEADS * NODE_BLOCKS], F32, name="total")
-            nc.vector.tensor_reduce(total[:], numerators[b][:].rearrange("p t m -> p m t"), AXIS.X, ALU.add)
-            inverse = small.tile([P, HEADS * NODE_BLOCKS], F32, name="inverse")
-            nc.vector.reciprocal(inverse[:], total[:])
-            p_by_node = small.tile([P, T, HEADS * NODE_BLOCKS], F32, name="p_by_node")
+            denominator = small.tile([P, GROUPS], F32, name="denominator")
+            nc.vector.tensor_reduce(denominator[:], numerators[b][:].rearrange("p t m -> p m t"), AXIS.X, ALU.add)
+            inverse = small.tile([P, GROUPS], F32, name="inverse")
+            nc.vector.reciprocal(inverse[:], denominator[:])
+            p_by_node = small.tile([P, T, GROUPS], F32, name="p_by_node")
             nc.vector.tensor_tensor(
-                p_by_node[:],
-                numerators[b][:],
-                inverse[:].unsqueeze(1).to_broadcast([P, T, HEADS * NODE_BLOCKS]),
-                ALU.mult,
+                p_by_node[:], numerators[b][:], inverse[:].unsqueeze(1).to_broadcast([P, T, GROUPS]), ALU.mult
             )
             p_flipped = flip_banks.tile([P, P], F32, tag="flipped")
             nc.tensor.transpose(p_flipped[:], p_by_node[:].rearrange("p t m -> p (t m)"), identity[:])
             p_rows = small.tile([P, P], F32, name="p_rows")
             nc.scalar.copy(p_rows[:], p_flipped[:])
             nc.scalar.dma_start(
-                out[b * P : b * P + T * HEADS, :].rearrange("r (k s) -> (r k) s", s=P), p_rows[:]
+                out[b * P : b * P + T * HEADS, :].rearrange("r (g s) -> (r g) s", s=P), p_rows[:]
             )
 
-        totals = {}
+        sum_banks = {}
+        u_of_neighbour_0 = {}
 
         def value_piece(b, t):
             if t == 0:
-                totals[b] = [banks.tile([P, BANK], F32, tag="bank", name="total_bank") for n in range(CHUNKS)]
+                sum_banks[b] = [banks.tile([P, BANK], F32, tag="bank", name="sum_bank") for n in range(CHUNKS)]
                 for n in range(CHUNKS):
-                    project_into_bank(totals[b][n], w1_sb, b * P, n, False)
+                    project_into_bank(sum_banks[b][n], w1_sb, b * P, n, False)
             p_spread = streamed.tile([P, S], F32, name="p_spread", tag="streamed")
             for h in range(HEADS):
                 nc.sync.dma_start(
                     p_spread[h * HALF : (h + 1) * HALF, :], out[b * P + t * HEADS + h, :].partition_broadcast(HALF)
                 )
             u = products.tile([P, S], F32, name="product")
-            nc.vector.tensor_tensor(
-                u[:],
-                projected["values", b][:].indirect(offsets[:, t * LIST_COLS : (t + 1) * LIST_COLS]),
-                p_spread[:],
-                ALU.mult,
-            )
-            for n in range(CHUNKS):
+            nc.vector.tensor_tensor(u[:], projected["values", b][:].indirect(list_of(t)), p_spread[:], ALU.mult)
+            if t == 0:
+                u_of_neighbour_0[b] = u
+            if t == 1:
+                pre_added = slice(0, PRE_ADDED * BANK)
+                nc.vector.tensor_tensor(u[:, pre_added], u_of_neighbour_0[b][:, pre_added], u[:, pre_added], ALU.add)
+            for n in range(PRE_ADDED if t == 0 else 0, CHUNKS):
                 nc.tensor.matmul(
-                    totals[b][n][:], identity[:], u[:, n * BANK : (n + 1) * BANK], start=False, stop=(t == T - 1)
+                    sum_banks[b][n][:], identity[:], u[:, n * BANK : (n + 1) * BANK], start=False, stop=(t == T - 1)
                 )
                 if t == T - 1:
                     result = results.tile([P, BANK], F32, name="result")
-                    nc.scalar.activation(
-                        result[:], totals[b][n][:], FUNC.Gelu, bias=bias[:, 2 * BLOCKS + b : 2 * BLOCKS + b + 1]
-                    )
+                    nc.scalar.activation(result[:], sum_banks[b][n][:], FUNC.Gelu, bias=bias_of(B1, b))
                     nc.scalar.dma_start(out[b * P : (b + 1) * P, n * BANK : (n + 1) * BANK], result[:])
 
-        rounds = [("keys", b) for b in range(BLOCKS)] + [("values", b) for b in range(BLOCKS)]
-
-        chunks_to_project = []
-        for kind, b in rounds:
-            for tile_kind in ("keys", "queries") if kind == "keys" else ("values",):
-                for n in range(CHUNKS):
-                    chunks_to_project.append((tile_kind, b, n))
-
-        first = 2 * CHUNKS
-        for kind, b, n in chunks_to_project[:first]:
+        tiles_in_order = [(kind, b) for b in range(BLOCKS) for kind in ("keys", "queries")]
+        tiles_in_order += [("values", b) for b in range(BLOCKS)]
+        chunks_in_order = [(kind, b, n) for kind, b in tiles_in_order for n in range(CHUNKS)]
+        at_once = 2 * CHUNKS
+        for kind, b, n in chunks_in_order[:at_once]:
             project_chunk(kind, b, n)
-        key_pieces_done = 0
-        for i, (kind, b) in enumerate(rounds):
+        for r in range(2 * BLOCKS):
             for t in range(T):
-                if kind == "keys":
-                    start = first + PER_PIECE * key_pieces_done
-                    for tile_kind, tile_b, n in chunks_to_project[start : start + PER_PIECE]:
-                        project_chunk(tile_kind, tile_b, n)
-                    key_piece(b, t)
-                    key_pieces_done += 1
+                if r < BLOCKS:
+                    first = at_once + PER_PIECE * (r * T + t)
+                    for kind, b, n in chunks_in_order[first : first + PER_PIECE]:
+                        project_chunk(kind, b, n)
+                    key_piece(r, t)
                 else:
-                    value_piece(b, t)
-                if i > 0 and rounds[i - 1][0] == "keys" and t == 1:
-                    softmax_shift(rounds[i - 1][1])
-                if i > 0 and rounds[i - 1][0] == "keys" and t == 3:
-                    softmax_normalise(rounds[i - 1][1])
+                    value_piece(r - BLOCKS, t)
+                if 1 <= r <= BLOCKS and t == 1:
+                    softmax_shift(r - 1)
+                if 1 <= r <= BLOCKS and t == 3:
+                    softmax_normalise(r - 1)

@@ -18,15 +18,16 @@ BLOCKS = C // P
 HEADS = 2
 HALF = P // HEADS
 BANK = 512
+PSUM_BANKS = 8
 CHUNKS = S // BANK
 NODE_BLOCKS = S // P
 GROUPS = HEADS * NODE_BLOCKS
 LIST_COLS = S // 16
 B0, QB, B1 = 0, 1, 2
 
+PER_BANK = BANK // P
 PER_PIECE = 3
-PRE_ADDED = 2
-STREAMED = 10
+STREAMED = 9
 
 FLOPS = 2 * C * S * 5 * C + 2 * C * T * S
 
@@ -42,17 +43,14 @@ def tile_attnno_b_kernel(tc, x, w0, b0, qw, qb, wkv, w1, b1, offs, out):
         products = ctx.enter_context(tc.tile_pool(name="products", bufs=3))
         rounded = ctx.enter_context(tc.tile_pool(name="rounded", bufs=2))
         results = ctx.enter_context(tc.tile_pool(name="results", bufs=CHUNKS))
+        flipped_sums = ctx.enter_context(tc.tile_pool(name="flipped_sums", bufs=2))
         small = ctx.enter_context(tc.tile_pool(name="small", bufs=2))
-        banks = ctx.enter_context(tc.psum_pool(name="banks", bufs=CHUNKS + 1))
-        score_banks = ctx.enter_context(tc.psum_pool(name="score_banks", bufs=2))
-        flip_banks = ctx.enter_context(tc.psum_pool(name="flip_banks", bufs=1))
+        banks = ctx.enter_context(tc.psum_pool(name="banks", bufs=PSUM_BANKS))
 
-        def load_weight(queue, w, name):
+        def load_weight(w, name):
             w_sb = held.tile([P, BLOCKS, w.shape[1]], BF16, name=name)
-            queue.dma_start(w_sb[:], w.rearrange("(k p) c -> p k c", p=P))
+            nc.sync.dma_start(w_sb[:], w.rearrange("(k p) c -> p k c", p=P))
             return w_sb
-
-        w0_sb = load_weight(nc.sync, w0, "w0_sb")
 
         bias_rows = held.tile([P, P], F32, name="bias_rows")
         nc.vector.memset(bias_rows[:], 0.0)
@@ -60,13 +58,10 @@ def tile_attnno_b_kernel(tc, x, w0, b0, qw, qb, wkv, w1, b1, offs, out):
             nc.scalar.dma_start(
                 bias_rows[which * BLOCKS : (which + 1) * BLOCKS, :], vec.rearrange("(b p) o -> b (p o)", p=P)
             )
-        wkv_sb = load_weight(nc.scalar, wkv, "wkv_sb")
-        qw_sb = load_weight(nc.scalar, qw, "qw_sb")
-        w1_sb = load_weight(nc.scalar, w1, "w1_sb")
 
         identity = held.tile([P, P], F32, name="identity")
         make_identity(nc, identity[:])
-        bias_flipped = flip_banks.tile([P, P], F32, tag="flipped")
+        bias_flipped = banks.tile([P, P], F32, tag="bank")
         nc.tensor.transpose(bias_flipped[:], bias_rows[:], identity[:])
         bias = held.tile([P, 3 * BLOCKS], F32, name="bias")
         nc.vector.tensor_copy(bias[:], bias_flipped[:, 0 : 3 * BLOCKS])
@@ -79,28 +74,33 @@ def tile_attnno_b_kernel(tc, x, w0, b0, qw, qb, wkv, w1, b1, offs, out):
         for h in range(HEADS):
             nc.vector.memset(head_sum[h * HALF : (h + 1) * HALF, h : h + 1], 0.125)
 
-        x_blocks = x.rearrange("(k p) s -> p k s", p=P)
+        w0_sb = held.tile([P, BLOCKS, C], BF16, name="w0_sb")
         x1 = [held.tile([P, BLOCKS, BANK], BF16, name=f"x1_{n}") for n in range(CHUNKS)]
         for n in range(CHUNKS):
             x_f32 = streamed.tile([P, BLOCKS, BANK], F32, name="x_f32", tag="streamed")
-            nc.sync.dma_start(x_f32[:], x_blocks[:, :, n * BANK : (n + 1) * BANK])
             x_bf = staged.tile([P, BLOCKS, BANK], BF16, name="x_bf")
+            x1_banks = [banks.tile([P, BANK], F32, tag="bank", name="x1_bank") for b in range(BLOCKS)]
             for k in range(BLOCKS):
+                if n == 0:
+                    nc.sync.dma_start(w0_sb[:, k, :], w0[k * P : (k + 1) * P, :])
+                nc.sync.dma_start(x_f32[:, k, :], x[k * P : (k + 1) * P, n * BANK : (n + 1) * BANK])
                 nc.vector.tensor_copy(x_bf[:, k, :], x_f32[:, k, :])
-            for b in range(BLOCKS):
-                bank = banks.tile([P, BANK], F32, tag="bank")
-                for k in range(BLOCKS):
+                for b in range(BLOCKS):
                     nc.tensor.matmul(
-                        bank[:],
+                        x1_banks[b][:],
                         w0_sb[:, k, b * P : (b + 1) * P],
                         x_bf[:, k, :],
                         start=(k == 0),
                         stop=(k == BLOCKS - 1),
                     )
-                nc.scalar.activation(x1[n][:, b, :], bank[:], FUNC.Gelu, bias=bias_of(B0, b))
+            for b in range(BLOCKS):
+                nc.scalar.activation(x1[n][:, b, :], x1_banks[b][:], FUNC.Gelu, bias=bias_of(B0, b))
 
+        wkv_sb = load_weight(wkv, "wkv_sb")
+        qw_sb = load_weight(qw, "qw_sb")
         offsets = held.tile([P, T * LIST_COLS], U16, name="offsets")
         nc.sync.dma_start(offsets[:], offs)
+        w1_sb = load_weight(w1, "w1_sb")
 
         def project_into_bank(bank, w_sb, first_col, n, stop):
             for k in range(BLOCKS):
@@ -121,7 +121,10 @@ def tile_attnno_b_kernel(tc, x, w0, b0, qw, qb, wkv, w1, b1, offs, out):
                 projected[kind, b] = windows.tile([P, S], F32, name="window")
             chunk = projected[kind, b][:, n * BANK : (n + 1) * BANK]
             bank = banks.tile([P, BANK], F32, tag="bank")
-            if kind == "keys":
+            if kind == "keys" and b == 0:
+                project_into_bank(bank, wkv_sb, b * P, n, True)
+                nc.vector.tensor_copy(chunk, bank[:])
+            elif kind == "keys":
                 project_into_bank(bank, wkv_sb, b * P, n, True)
                 nc.scalar.copy(chunk, bank[:])
             elif kind == "values":
@@ -131,25 +134,30 @@ def tile_attnno_b_kernel(tc, x, w0, b0, qw, qb, wkv, w1, b1, offs, out):
                 project_into_bank(bank, qw_sb, b * P, n, True)
                 nc.scalar.activation(chunk, bank[:], FUNC.Identity, bias=bias_of(QB, b))
 
-        def list_of(t):
-            return offsets[:, t * LIST_COLS : (t + 1) * LIST_COLS]
+        def list_of(t, nodes):
+            return offsets[:, (t * S + nodes.start) // 16 : (t * S + nodes.stop) // 16]
 
         scores = {}
 
-        def key_piece(b, t):
+        def key_piece(b, t, width):
             if t == 0:
-                scores[b] = score_banks.tile([P, T * GROUPS], F32, name="scores")
+                scores[b] = banks.tile([P, T * GROUPS], F32, tag="bank", name="scores")
             e = products.tile([P, S], F32, name="product")
-            nc.vector.tensor_tensor(
-                e[:], projected["keys", b][:].indirect(list_of(t)), projected["queries", b][:], ALU.mult
-            )
             e_bf = rounded.tile([P, S], BF16, name="e_bf")
-            nc.scalar.copy(e_bf[:], e[:])
             by_node_block = scores[b][:].rearrange("p (t h g) -> p t g h", t=T, h=HEADS)
-            for g in range(NODE_BLOCKS):
-                nc.tensor.matmul(
-                    by_node_block[:, t, g, :], e_bf[:, g * P : (g + 1) * P], head_sum[:], start=True, stop=True
+            for first in range(0, S, width):
+                nodes = slice(first, first + width)
+                nc.vector.tensor_tensor(
+                    e[:, nodes],
+                    projected["keys", b][:].indirect(list_of(t, nodes)),
+                    projected["queries", b][:, nodes],
+                    ALU.mult,
                 )
+                nc.scalar.copy(e_bf[:, nodes], e[:, nodes])
+                for g in range(nodes.start // P, nodes.stop // P):
+                    nc.tensor.matmul(
+                        by_node_block[:, t, g, :], e_bf[:, g * P : (g + 1) * P], head_sum[:], start=True, stop=True
+                    )
 
         numerators = {}
 
@@ -175,7 +183,7 @@ def tile_attnno_b_kernel(tc, x, w0, b0, qw, qb, wkv, w1, b1, offs, out):
             nc.vector.tensor_tensor(
                 p_by_node[:], numerators[b][:], inverse[:].unsqueeze(1).to_broadcast([P, T, GROUPS]), ALU.mult
             )
-            p_flipped = flip_banks.tile([P, P], F32, tag="flipped")
+            p_flipped = banks.tile([P, P], F32, tag="bank")
             nc.tensor.transpose(p_flipped[:], p_by_node[:].rearrange("p t m -> p (t m)"), identity[:])
             p_rows = small.tile([P, P], F32, name="p_rows")
             nc.scalar.copy(p_rows[:], p_flipped[:])
@@ -183,34 +191,53 @@ def tile_attnno_b_kernel(tc, x, w0, b0, qw, qb, wkv, w1, b1, offs, out):
                 out[b * P : b * P + T * HEADS, :].rearrange("r (g s) -> (r g) s", s=P), p_rows[:]
             )
 
-        sum_banks = {}
-        u_of_neighbour_0 = {}
+        sums = {}
 
-        def value_piece(b, t):
+        def value_piece(b, t, width):
             if t == 0:
-                sum_banks[b] = [banks.tile([P, BANK], F32, tag="bank", name="sum_bank") for n in range(CHUNKS)]
-                for n in range(CHUNKS):
-                    project_into_bank(sum_banks[b][n], w1_sb, b * P, n, False)
+                sums[b] = [banks.tile([P, BANK], F32, tag="bank", name="sum_bank") for n in range(CHUNKS)]
             p_spread = streamed.tile([P, S], F32, name="p_spread", tag="streamed")
             for h in range(HEADS):
                 nc.sync.dma_start(
                     p_spread[h * HALF : (h + 1) * HALF, :], out[b * P + t * HEADS + h, :].partition_broadcast(HALF)
                 )
             u = products.tile([P, S], F32, name="product")
-            nc.vector.tensor_tensor(u[:], projected["values", b][:].indirect(list_of(t)), p_spread[:], ALU.mult)
-            if t == 0:
-                u_of_neighbour_0[b] = u
-            if t == 1:
-                pre_added = slice(0, PRE_ADDED * BANK)
-                nc.vector.tensor_tensor(u[:, pre_added], u_of_neighbour_0[b][:, pre_added], u[:, pre_added], ALU.add)
-            for n in range(PRE_ADDED if t == 0 else 0, CHUNKS):
-                nc.tensor.matmul(
-                    sum_banks[b][n][:], identity[:], u[:, n * BANK : (n + 1) * BANK], start=False, stop=(t == T - 1)
+            for first in range(0, S, width):
+                nodes = slice(first, first + width)
+                nc.vector.tensor_tensor(
+                    u[:, nodes], projected["values", b][:].indirect(list_of(t, nodes)), p_spread[:, nodes], ALU.mult
                 )
+                for g in range(nodes.start // P, nodes.stop // P):
+                    n, place = divmod(g, PER_BANK)
+                    nc.tensor.matmul(
+                        sums[b][n][:, place * P : (place + 1) * P],
+                        u[:, g * P : (g + 1) * P],
+                        identity[:],
+                        is_transpose=True,
+                        start=(t == 0 and place == 0),
+                        stop=(t == T - 1 and place == PER_BANK - 1),
+                    )
                 if t == T - 1:
-                    result = results.tile([P, BANK], F32, name="result")
-                    nc.scalar.activation(result[:], sum_banks[b][n][:], FUNC.Gelu, bias=bias_of(B1, b))
-                    nc.scalar.dma_start(out[b * P : (b + 1) * P, n * BANK : (n + 1) * BANK], result[:])
+                    for n in range(nodes.start // BANK, nodes.stop // BANK):
+                        finish_chunk(b, n)
+
+        def finish_chunk(b, n):
+            flipped_sum = flipped_sums.tile([P, BANK], F32, name="flipped_sum")
+            nc.scalar.copy(flipped_sum[:], sums[b][n][:])
+            bank = banks.tile([P, BANK], F32, tag="bank")
+            project_into_bank(bank, w1_sb, b * P, n, False)
+            for place in range(PER_BANK):
+                nc.tensor.matmul(
+                    bank[:, place * P : (place + 1) * P],
+                    flipped_sum[:, place * P : (place + 1) * P],
+                    identity[:],
+                    is_transpose=True,
+                    start=False,
+                    stop=(place == PER_BANK - 1),
+                )
+            result = results.tile([P, BANK], F32, name="result")
+            nc.scalar.activation(result[:], bank[:], FUNC.Gelu, bias=bias_of(B1, b))
+            nc.scalar.dma_start(out[b * P : (b + 1) * P, n * BANK : (n + 1) * BANK], result[:])
 
         tiles_in_order = [(kind, b) for b in range(BLOCKS) for kind in ("keys", "queries")]
         tiles_in_order += [("values", b) for b in range(BLOCKS)]
@@ -224,9 +251,9 @@ def tile_attnno_b_kernel(tc, x, w0, b0, qw, qb, wkv, w1, b1, offs, out):
                     first = at_once + PER_PIECE * (r * T + t)
                     for kind, b, n in chunks_in_order[first : first + PER_PIECE]:
                         project_chunk(kind, b, n)
-                    key_piece(r, t)
+                    key_piece(r, t, BANK if (r, t) == (0, 0) else S)
                 else:
-                    value_piece(r - BLOCKS, t)
+                    value_piece(r - BLOCKS, t, BANK if (r, t) == (2 * BLOCKS - 1, T - 1) else S)
                 if 1 <= r <= BLOCKS and t == 1:
                     softmax_shift(r - 1)
                 if 1 <= r <= BLOCKS and t == 3:

@@ -52,22 +52,15 @@ def tile_attnno_b_kernel(tc, x, w0, b0, qw, qb, wkv, w1, b1, offs, out):
             nc.sync.dma_start(w_sb[:], w.rearrange("(k p) c -> p k c", p=P))
             return w_sb
 
-        bias_rows = held.tile([P, P], F32, name="bias_rows")
-        nc.vector.memset(bias_rows[:], 0.0)
+        biases = [held.tile([P, BLOCKS], F32, name=f"bias_{which}") for which in (B0, QB, B1)]
         for which, vec in enumerate((b0, qb, b1)):
-            nc.scalar.dma_start(
-                bias_rows[which * BLOCKS : (which + 1) * BLOCKS, :], vec.rearrange("(b p) o -> b (p o)", p=P)
-            )
+            nc.scalar.dma_start(biases[which][:], vec.rearrange("(b p) o -> p (b o)", p=P))
+
+        def bias_of(which, b):
+            return biases[which][:, b : b + 1]
 
         identity = held.tile([P, P], F32, name="identity")
         make_identity(nc, identity[:])
-        bias_flipped = banks.tile([P, P], F32, tag="bank")
-        nc.tensor.transpose(bias_flipped[:], bias_rows[:], identity[:])
-        bias = held.tile([P, 3 * BLOCKS], F32, name="bias")
-        nc.vector.tensor_copy(bias[:], bias_flipped[:, 0 : 3 * BLOCKS])
-
-        def bias_of(which, b):
-            return bias[:, which * BLOCKS + b : which * BLOCKS + b + 1]
 
         head_sum = held.tile([P, HEADS], BF16, name="head_sum")
         nc.vector.memset(head_sum[:], 0.0)

@@ -45,6 +45,7 @@ def tile_attnno_b_kernel(tc, x, w0, b0, qw, qb, wkv, w1, b1, offs, out):
         results = ctx.enter_context(tc.tile_pool(name="results", bufs=CHUNKS))
         flipped_sums = ctx.enter_context(tc.tile_pool(name="flipped_sums", bufs=2))
         small = ctx.enter_context(tc.tile_pool(name="small", bufs=2))
+        kept = ctx.enter_context(tc.tile_pool(name="kept", bufs=BLOCKS))
         banks = ctx.enter_context(tc.psum_pool(name="banks", bufs=PSUM_BANKS))
 
         def load_weight(w, name):
@@ -154,7 +155,7 @@ def tile_attnno_b_kernel(tc, x, w0, b0, qw, qb, wkv, w1, b1, offs, out):
 
         numerators = {}
 
-        def softmax_shift(b):
+        def softmax_numerators(b):
             top = small.tile([P, GROUPS], F32, name="top")
             nc.vector.tensor_reduce(top[:], scores[b][:].rearrange("p (t m) -> p m t", t=T), AXIS.X, ALU.max)
             shifted = small.tile([P, T, GROUPS], F32, name="shifted")
@@ -166,39 +167,35 @@ def tile_attnno_b_kernel(tc, x, w0, b0, qw, qb, wkv, w1, b1, offs, out):
             )
             numerators[b] = small.tile([P, T, GROUPS], F32, name="numerator")
             nc.scalar.activation(numerators[b][:], shifted[:], FUNC.Exp)
+            flipped = banks.tile([P, P], F32, tag="bank")
+            nc.tensor.transpose(flipped[:], numerators[b][:].rearrange("p t m -> p (t m)"), identity[:])
+            rows = small.tile([P, P], F32, name="rows")
+            nc.scalar.copy(rows[:], flipped[:])
+            nc.scalar.dma_start(out[b * P : b * P + T * HEADS, :].rearrange("r (g s) -> (r g) s", s=P), rows[:])
 
-        def softmax_normalise(b):
+        inverses = {}
+
+        def softmax_inverses(b):
             denominator = small.tile([P, GROUPS], F32, name="denominator")
             nc.vector.tensor_reduce(denominator[:], numerators[b][:].rearrange("p t m -> p m t"), AXIS.X, ALU.add)
-            inverse = small.tile([P, GROUPS], F32, name="inverse")
-            nc.vector.reciprocal(inverse[:], denominator[:])
-            p_by_node = small.tile([P, T, GROUPS], F32, name="p_by_node")
-            nc.vector.tensor_tensor(
-                p_by_node[:], numerators[b][:], inverse[:].unsqueeze(1).to_broadcast([P, T, GROUPS]), ALU.mult
-            )
-            p_flipped = banks.tile([P, P], F32, tag="bank")
-            nc.tensor.transpose(p_flipped[:], p_by_node[:].rearrange("p t m -> p (t m)"), identity[:])
-            p_rows = small.tile([P, P], F32, name="p_rows")
-            nc.scalar.copy(p_rows[:], p_flipped[:])
-            nc.scalar.dma_start(
-                out[b * P : b * P + T * HEADS, :].rearrange("r (g s) -> (r g) s", s=P), p_rows[:]
-            )
+            inverses[b] = kept.tile([P, GROUPS], F32, name="inverse")
+            nc.vector.reciprocal(inverses[b][:], denominator[:])
 
         sums = {}
 
         def value_piece(b, t, width):
             if t == 0:
                 sums[b] = [banks.tile([P, BANK], F32, tag="bank", name="sum_bank") for n in range(CHUNKS)]
-            p_spread = streamed.tile([P, S], F32, name="p_spread", tag="streamed")
+            spread = streamed.tile([P, S], F32, name="spread", tag="streamed")
             for h in range(HEADS):
                 nc.sync.dma_start(
-                    p_spread[h * HALF : (h + 1) * HALF, :], out[b * P + t * HEADS + h, :].partition_broadcast(HALF)
+                    spread[h * HALF : (h + 1) * HALF, :], out[b * P + t * HEADS + h, :].partition_broadcast(HALF)
                 )
             u = products.tile([P, S], F32, name="product")
             for first in range(0, S, width):
                 nodes = slice(first, first + width)
                 nc.vector.tensor_tensor(
-                    u[:, nodes], projected["values", b][:].indirect(list_of(t, nodes)), p_spread[:, nodes], ALU.mult
+                    u[:, nodes], projected["values", b][:].indirect(list_of(t, nodes)), spread[:, nodes], ALU.mult
                 )
                 for g in range(nodes.start // P, nodes.stop // P):
                     n, place = divmod(g, PER_BANK)
@@ -216,7 +213,13 @@ def tile_attnno_b_kernel(tc, x, w0, b0, qw, qb, wkv, w1, b1, offs, out):
 
         def finish_chunk(b, n):
             flipped_sum = flipped_sums.tile([P, BANK], F32, name="flipped_sum")
-            nc.scalar.copy(flipped_sum[:], sums[b][n][:])
+            for place in range(PER_BANK):
+                for h in range(HEADS):
+                    m = h * NODE_BLOCKS + n * PER_BANK + place
+                    head = slice(place * P + h * HALF, place * P + (h + 1) * HALF)
+                    nc.scalar.activation(
+                        flipped_sum[:, head], sums[b][n][:, head], FUNC.Copy, scale=inverses[b][:, m : m + 1]
+                    )
             bank = banks.tile([P, BANK], F32, tag="bank")
             project_into_bank(bank, w1_sb, b * P, n, False)
             for place in range(PER_BANK):
@@ -247,7 +250,7 @@ def tile_attnno_b_kernel(tc, x, w0, b0, qw, qb, wkv, w1, b1, offs, out):
                     key_piece(r, t, BANK if (r, t) == (0, 0) else S)
                 else:
                     value_piece(r - BLOCKS, t, BANK if (r, t) == (2 * BLOCKS - 1, T - 1) else S)
+                if 2 <= r <= BLOCKS + 1 and t == 1:
+                    softmax_inverses(r - 2)
                 if 1 <= r <= BLOCKS and t == 1:
-                    softmax_shift(r - 1)
-                if 1 <= r <= BLOCKS and t == 3:
-                    softmax_normalise(r - 1)
+                    softmax_numerators(r - 1)

@@ -250,7 +250,7 @@ def tile_attnno_b_kernel(tc, x, w0, b0, qw, qb, wkv, w1, b1, offs, out):
                     key_piece(r, t, BANK if (r, t) == (0, 0) else S)
                 else:
                     value_piece(r - BLOCKS, t, BANK if (r, t) == (2 * BLOCKS - 1, T - 1) else S)
-                if 2 <= r <= BLOCKS + 1 and t == 1:
+                if 2 <= r <= BLOCKS + 1 and t == 2:
                     softmax_inverses(r - 2)
-                if 1 <= r <= BLOCKS and t == 1:
+                if 1 <= r <= BLOCKS and t == 2:
                     softmax_numerators(r - 1)

@@ -54,14 +54,18 @@ def tile_attnno_b_kernel(tc, x, w0, b0, qw, qb, wkv, w1, b1, offs, out):
             return w_sb
 
         biases = [held.tile([P, BLOCKS], F32, name=f"bias_{which}") for which in (B0, QB, B1)]
-        for which, vec in enumerate((b0, qb, b1)):
-            nc.scalar.dma_start(biases[which][:], vec.rearrange("(b p) o -> p (b o)", p=P))
+
+        def load_biases():
+            for which, vec in enumerate((b0, qb, b1)):
+                nc.scalar.dma_start(biases[which][:], vec.rearrange("(b p) o -> p (b o)", p=P))
 
         def bias_of(which, b):
             return biases[which][:, b : b + 1]
 
         identity = held.tile([P, P], F32, name="identity")
         make_identity(nc, identity[:])
+        same_group = held.tile([P, GROUPS], F32, name="same_group")
+        nc.vector.tensor_reduce(same_group[:], identity[:].rearrange("p (t m) -> p m t", t=T), AXIS.X, ALU.add)
 
         head_sum = held.tile([P, HEADS], BF16, name="head_sum")
         nc.vector.memset(head_sum[:], 0.0)
@@ -76,7 +80,7 @@ def tile_attnno_b_kernel(tc, x, w0, b0, qw, qb, wkv, w1, b1, offs, out):
             x1_banks = [banks.tile([P, BANK], F32, tag="bank", name="x1_bank") for b in range(BLOCKS)]
             for k in range(BLOCKS):
                 if n == 0:
-                    nc.sync.dma_start(w0_sb[:, k, :], w0[k * P : (k + 1) * P, :])
+                    nc.scalar.dma_start(w0_sb[:, k, :], w0[k * P : (k + 1) * P, :])
                 nc.sync.dma_start(x_f32[:, k, :], x[k * P : (k + 1) * P, n * BANK : (n + 1) * BANK])
                 nc.vector.tensor_copy(x_bf[:, k, :], x_f32[:, k, :])
                 for b in range(BLOCKS):
@@ -87,6 +91,8 @@ def tile_attnno_b_kernel(tc, x, w0, b0, qw, qb, wkv, w1, b1, offs, out):
                         start=(k == 0),
                         stop=(k == BLOCKS - 1),
                     )
+            if n == 0:
+                load_biases()
             for b in range(BLOCKS):
                 nc.scalar.activation(x1[n][:, b, :], x1_banks[b][:], FUNC.Gelu, bias=bias_of(B0, b))
 
@@ -154,6 +160,7 @@ def tile_attnno_b_kernel(tc, x, w0, b0, qw, qb, wkv, w1, b1, offs, out):
                     )
 
         numerators = {}
+        denominators = {}
 
         def softmax_numerators(b):
             top = small.tile([P, GROUPS], F32, name="top")
@@ -172,14 +179,16 @@ def tile_attnno_b_kernel(tc, x, w0, b0, qw, qb, wkv, w1, b1, offs, out):
             rows = small.tile([P, P], F32, name="rows")
             nc.scalar.copy(rows[:], flipped[:])
             nc.scalar.dma_start(out[b * P : b * P + T * HEADS, :].rearrange("r (g s) -> (r g) s", s=P), rows[:])
+            summed = banks.tile([P, GROUPS], F32, tag="bank")
+            nc.tensor.matmul(summed[:], rows[:], same_group[:], start=True, stop=True)
+            denominators[b] = small.tile([P, GROUPS], F32, name="denominator")
+            nc.scalar.copy(denominators[b][:], summed[:])
 
         inverses = {}
 
         def softmax_inverses(b):
-            denominator = small.tile([P, GROUPS], F32, name="denominator")
-            nc.vector.tensor_reduce(denominator[:], numerators[b][:].rearrange("p t m -> p m t"), AXIS.X, ALU.add)
             inverses[b] = kept.tile([P, GROUPS], F32, name="inverse")
-            nc.vector.reciprocal(inverses[b][:], denominator[:])
+            nc.vector.reciprocal(inverses[b][:], denominators[b][:])
 
         sums = {}
 

@@ -18,6 +18,7 @@ BLOCKS = C // P
 HEADS = 2
 HALF = P // HEADS
 BANK = 512
+HALF_BANK = BANK // 2
 PSUM_BANKS = 8
 CHUNKS = S // BANK
 NODE_BLOCKS = S // P
@@ -26,7 +27,6 @@ LIST_COLS = S // 16
 B0, QB, B1 = 0, 1, 2
 
 PER_BANK = BANK // P
-PER_PIECE = 3
 STREAMED = 9
 
 FLOPS = 2 * C * S * 5 * C + 2 * C * T * S
@@ -38,15 +38,15 @@ def tile_attnno_b_kernel(tc, x, w0, b0, qw, qb, wkv, w1, b1, offs, out):
         held = ctx.enter_context(tc.tile_pool(name="held", bufs=1))
         streamed = ctx.enter_context(tc.tile_pool(name="streamed", bufs=STREAMED))
         staged = ctx.enter_context(tc.tile_pool(name="staged", bufs=2))
-        windows = ctx.enter_context(tc.tile_pool(name="windows", bufs=BLOCKS + 1))
+        windows = ctx.enter_context(tc.tile_pool(name="windows", bufs=3))
         queries = ctx.enter_context(tc.tile_pool(name="queries", bufs=3))
-        products = ctx.enter_context(tc.tile_pool(name="products", bufs=3))
+        products = ctx.enter_context(tc.tile_pool(name="products", bufs=6))
         rounded = ctx.enter_context(tc.tile_pool(name="rounded", bufs=2))
         results = ctx.enter_context(tc.tile_pool(name="results", bufs=CHUNKS))
         flipped_sums = ctx.enter_context(tc.tile_pool(name="flipped_sums", bufs=2))
         small = ctx.enter_context(tc.tile_pool(name="small", bufs=2))
         kept = ctx.enter_context(tc.tile_pool(name="kept", bufs=BLOCKS))
-        banks = ctx.enter_context(tc.psum_pool(name="banks", bufs=PSUM_BANKS))
+        banks = [ctx.enter_context(tc.psum_pool(name=f"banks_{i}", bufs=PSUM_BANKS // 2)) for i in range(2)]
 
         def load_weight(w, name):
             w_sb = held.tile([P, BLOCKS, w.shape[1]], BF16, name=name)
@@ -64,37 +64,58 @@ def tile_attnno_b_kernel(tc, x, w0, b0, qw, qb, wkv, w1, b1, offs, out):
 
         identity = held.tile([P, P], F32, name="identity")
         make_identity(nc, identity[:])
-        same_group = held.tile([P, GROUPS], F32, name="same_group")
-        nc.vector.tensor_reduce(same_group[:], identity[:].rearrange("p (t m) -> p m t", t=T), AXIS.X, ALU.add)
-
-        head_sum = held.tile([P, HEADS], BF16, name="head_sum")
-        nc.vector.memset(head_sum[:], 0.0)
-        for h in range(HEADS):
-            nc.vector.memset(head_sum[h * HALF : (h + 1) * HALF, h : h + 1], 0.125)
 
         w0_sb = held.tile([P, BLOCKS, C], BF16, name="w0_sb")
         x1 = [held.tile([P, BLOCKS, BANK], BF16, name=f"x1_{n}") for n in range(CHUNKS)]
         for n in range(CHUNKS):
             x_f32 = streamed.tile([P, BLOCKS, BANK], F32, name="x_f32", tag="streamed")
             x_bf = staged.tile([P, BLOCKS, BANK], BF16, name="x_bf")
-            x1_banks = [banks.tile([P, BANK], F32, tag="bank", name="x1_bank") for b in range(BLOCKS)]
+            x1_banks = [banks[n % 2].tile([P, BANK], F32, tag="bank", name="x1_bank") for b in range(BLOCKS)]
             for k in range(BLOCKS):
                 if n == 0:
                     nc.scalar.dma_start(w0_sb[:, k, :], w0[k * P : (k + 1) * P, :])
-                nc.sync.dma_start(x_f32[:, k, :], x[k * P : (k + 1) * P, n * BANK : (n + 1) * BANK])
-                nc.vector.tensor_copy(x_bf[:, k, :], x_f32[:, k, :])
-                for b in range(BLOCKS):
-                    nc.tensor.matmul(
-                        x1_banks[b][:],
-                        w0_sb[:, k, b * P : (b + 1) * P],
-                        x_bf[:, k, :],
-                        start=(k == 0),
-                        stop=(k == BLOCKS - 1),
+                width = HALF_BANK if n == 0 and k == 0 else BANK
+                for first in range(0, BANK, width):
+                    cols = slice(first, first + width)
+                    nc.sync.dma_start(
+                        x_f32[:, k, cols], x[k * P : (k + 1) * P, n * BANK + first : n * BANK + first + width]
                     )
+                    nc.vector.tensor_copy(x_bf[:, k, cols], x_f32[:, k, cols])
+                    for b in range(BLOCKS):
+                        nc.tensor.matmul(
+                            x1_banks[b][:, cols],
+                            w0_sb[:, k, b * P : (b + 1) * P],
+                            x_bf[:, k, cols],
+                            start=(k == 0 and first == 0),
+                            stop=(k == BLOCKS - 1),
+                        )
             if n == 0:
                 load_biases()
             for b in range(BLOCKS):
                 nc.scalar.activation(x1[n][:, b, :], x1_banks[b][:], FUNC.Gelu, bias=bias_of(B0, b))
+
+        last_row = P - NODE_BLOCKS - 1
+        strip = held.tile([P, last_row + P], BF16, name="strip")
+        nc.vector.memset(strip[:], 0.0)
+        for h in range(HEADS):
+            column = last_row + h * NODE_BLOCKS
+            nc.vector.memset(strip[h * HALF : (h + 1) * HALF, column : column + 1], 0.125)
+
+        def head_sum_of(t, g):
+            start = last_row - (t * GROUPS + g)
+            return strip[:, start : start + P]
+
+        def rows_of(t):
+            return slice(t * GROUPS, (t + 1) * GROUPS)
+
+        over_1 = held.tile([P, P], F32, name="over_1")
+        over_2 = held.tile([P, P], F32, name="over_2")
+        for t in range(T):
+            own = identity[:, rows_of(t)]
+            nc.vector.tensor_tensor(over_1[:, rows_of(t)], identity[:, rows_of(t ^ 1)], own, ALU.subtract)
+            nc.vector.tensor_tensor(over_2[:, rows_of(t)], identity[:, rows_of(t ^ 2)], own, ALU.subtract)
+        same_m = held.tile([P, GROUPS], F32, name="same_m")
+        nc.vector.tensor_reduce(same_m[:], identity[:].rearrange("p (t m) -> p m t", t=T), AXIS.X, ALU.add)
 
         wkv_sb = load_weight(wkv, "wkv_sb")
         qw_sb = load_weight(qw, "qw_sb")
@@ -102,51 +123,52 @@ def tile_attnno_b_kernel(tc, x, w0, b0, qw, qb, wkv, w1, b1, offs, out):
         nc.sync.dma_start(offsets[:], offs)
         w1_sb = load_weight(w1, "w1_sb")
 
-        def project_into_bank(bank, w_sb, first_col, n, stop):
+        def project_into_bank(bank, w_sb, first_col, nodes, stop):
+            n, place = divmod(nodes.start, BANK)
+            width = nodes.stop - nodes.start
             for k in range(BLOCKS):
                 nc.tensor.matmul(
-                    bank[:],
+                    bank[:, 0:width],
                     w_sb[:, k, first_col : first_col + P],
-                    x1[n][:, k, :],
+                    x1[n][:, k, place : place + width],
                     start=(k == 0),
                     stop=(stop and k == BLOCKS - 1),
                 )
 
         projected = {}
 
-        def project_chunk(kind, b, n):
-            if n == 0 and kind == "queries":
+        def project(kind, b, nodes, ring):
+            if nodes.start == 0 and kind == "queries":
                 projected[kind, b] = queries.tile([P, S], F32, name="q")
-            elif n == 0:
+            elif nodes.start == 0:
                 projected[kind, b] = windows.tile([P, S], F32, name="window")
-            chunk = projected[kind, b][:, n * BANK : (n + 1) * BANK]
-            bank = banks.tile([P, BANK], F32, tag="bank")
+            chunk = projected[kind, b][:, nodes]
+            bank = banks[ring].tile([P, BANK], F32, tag="bank")
+            made = bank[:, 0 : nodes.stop - nodes.start]
             if kind == "keys" and b == 0:
-                project_into_bank(bank, wkv_sb, b * P, n, True)
-                nc.vector.tensor_copy(chunk, bank[:])
+                project_into_bank(bank, wkv_sb, b * P, nodes, True)
+                nc.vector.tensor_copy(chunk, made)
             elif kind == "keys":
-                project_into_bank(bank, wkv_sb, b * P, n, True)
-                nc.scalar.copy(chunk, bank[:])
+                project_into_bank(bank, wkv_sb, b * P, nodes, True)
+                nc.scalar.copy(chunk, made)
             elif kind == "values":
-                project_into_bank(bank, wkv_sb, C + b * P, n, True)
-                nc.scalar.copy(chunk, bank[:])
+                project_into_bank(bank, wkv_sb, C + b * P, nodes, True)
+                nc.scalar.copy(chunk, made)
             else:
-                project_into_bank(bank, qw_sb, b * P, n, True)
-                nc.scalar.activation(chunk, bank[:], FUNC.Identity, bias=bias_of(QB, b))
+                project_into_bank(bank, qw_sb, b * P, nodes, True)
+                nc.scalar.activation(chunk, made, FUNC.Identity, bias=bias_of(QB, b))
 
         def list_of(t, nodes):
             return offsets[:, (t * S + nodes.start) // 16 : (t * S + nodes.stop) // 16]
 
         scores = {}
 
-        def key_piece(b, t, width):
+        def key_piece(b, t, runs):
             if t == 0:
-                scores[b] = banks.tile([P, T * GROUPS], F32, tag="bank", name="scores")
+                scores[b] = banks[1].tile([P, P], F32, tag="bank", name="scores")
             e = products.tile([P, S], F32, name="product")
             e_bf = rounded.tile([P, S], BF16, name="e_bf")
-            by_node_block = scores[b][:].rearrange("p (t h g) -> p t g h", t=T, h=HEADS)
-            for first in range(0, S, width):
-                nodes = slice(first, first + width)
+            for nodes in runs:
                 nc.vector.tensor_tensor(
                     e[:, nodes],
                     projected["keys", b][:].indirect(list_of(t, nodes)),
@@ -156,110 +178,142 @@ def tile_attnno_b_kernel(tc, x, w0, b0, qw, qb, wkv, w1, b1, offs, out):
                 nc.scalar.copy(e_bf[:, nodes], e[:, nodes])
                 for g in range(nodes.start // P, nodes.stop // P):
                     nc.tensor.matmul(
-                        by_node_block[:, t, g, :], e_bf[:, g * P : (g + 1) * P], head_sum[:], start=True, stop=True
+                        scores[b][:],
+                        head_sum_of(t, g),
+                        e_bf[:, g * P : (g + 1) * P],
+                        start=(t == 0 and g == 0),
+                        stop=(t == T - 1 and g == NODE_BLOCKS - 1),
                     )
 
         numerators = {}
-        denominators = {}
+
+        def add_up(terms):
+            total = banks[1].tile([P, P], F32, tag="bank", name="total")
+            for i, (stationary, moving) in enumerate(terms):
+                nc.tensor.matmul(total[:], stationary[:], moving[:], start=(i == 0), stop=(i == len(terms) - 1))
+            return total
 
         def softmax_numerators(b):
-            top = small.tile([P, GROUPS], F32, name="top")
-            nc.vector.tensor_reduce(top[:], scores[b][:].rearrange("p (t m) -> p m t", t=T), AXIS.X, ALU.max)
-            shifted = small.tile([P, T, GROUPS], F32, name="shifted")
-            nc.vector.tensor_tensor(
-                shifted[:],
-                scores[b][:].rearrange("p (t m) -> p t m", t=T),
-                top[:].unsqueeze(1).to_broadcast([P, T, GROUPS]),
-                ALU.subtract,
+            score = small.tile([P, P], F32, name="score")
+            nc.scalar.copy(score[:], scores[b][:])
+            up_1 = small.tile([P, P], F32, name="up_1")
+            nc.scalar.activation(up_1[:], add_up([(over_1, score)])[:], FUNC.Relu)
+            up_2 = small.tile([P, P], F32, name="up_2")
+            nc.scalar.activation(up_2[:], add_up([(over_2, score), (over_2, up_1)])[:], FUNC.Relu)
+            numerators[b] = small.tile([P, P], F32, name="numerator")
+            below = add_up([(identity, up_1), (identity, up_2)])
+            nc.scalar.activation(numerators[b][:], below[:], FUNC.Exp, scale=-1.0)
+            nc.scalar.dma_start(
+                out[b * P : b * P + T * HEADS, :].rearrange("r (g s) -> (r g) s", s=P), numerators[b][:]
             )
-            numerators[b] = small.tile([P, T, GROUPS], F32, name="numerator")
-            nc.scalar.activation(numerators[b][:], shifted[:], FUNC.Exp)
-            flipped = banks.tile([P, P], F32, tag="bank")
-            nc.tensor.transpose(flipped[:], numerators[b][:].rearrange("p t m -> p (t m)"), identity[:])
-            rows = small.tile([P, P], F32, name="rows")
-            nc.scalar.copy(rows[:], flipped[:])
-            nc.scalar.dma_start(out[b * P : b * P + T * HEADS, :].rearrange("r (g s) -> (r g) s", s=P), rows[:])
-            summed = banks.tile([P, GROUPS], F32, tag="bank")
-            nc.tensor.matmul(summed[:], rows[:], same_group[:], start=True, stop=True)
-            denominators[b] = small.tile([P, GROUPS], F32, name="denominator")
-            nc.scalar.copy(denominators[b][:], summed[:])
 
         inverses = {}
 
         def softmax_inverses(b):
+            summed = banks[1].tile([P, GROUPS], F32, tag="bank", name="summed")
+            nc.tensor.matmul(summed[:], numerators[b][:], same_m[:], start=True, stop=True)
             inverses[b] = kept.tile([P, GROUPS], F32, name="inverse")
-            nc.vector.reciprocal(inverses[b][:], denominators[b][:])
+            nc.vector.reciprocal(inverses[b][:], summed[:])
 
-        sums = {}
+        def spread_numerators(b):
+            spreads = [streamed.tile([P, S], F32, name="spread", tag="streamed") for t in range(T)]
+            for t in range(T):
+                for h in range(HEADS):
+                    nc.sync.dma_start(
+                        spreads[t][h * HALF : (h + 1) * HALF, :], out[b * P + t * HEADS + h, :].partition_broadcast(HALF)
+                    )
+            return spreads
 
-        def value_piece(b, t, width):
-            if t == 0:
-                sums[b] = [banks.tile([P, BANK], F32, tag="bank", name="sum_bank") for n in range(CHUNKS)]
-            spread = streamed.tile([P, S], F32, name="spread", tag="streamed")
-            for h in range(HEADS):
-                nc.sync.dma_start(
-                    spread[h * HALF : (h + 1) * HALF, :], out[b * P + t * HEADS + h, :].partition_broadcast(HALF)
-                )
+        def value_look_up(b, t, nodes, spread, parts, sums):
             u = products.tile([P, S], F32, name="product")
-            for first in range(0, S, width):
-                nodes = slice(first, first + width)
-                nc.vector.tensor_tensor(
-                    u[:, nodes], projected["values", b][:].indirect(list_of(t, nodes)), spread[:, nodes], ALU.mult
-                )
-                for g in range(nodes.start // P, nodes.stop // P):
-                    n, place = divmod(g, PER_BANK)
+            nc.vector.tensor_tensor(
+                u[:, nodes], projected["values", b][:].indirect(list_of(t, nodes)), spread[:, nodes], ALU.mult
+            )
+            for part, bank in zip(parts, sums):
+                for first in range(part.start, part.stop, P):
                     nc.tensor.matmul(
-                        sums[b][n][:, place * P : (place + 1) * P],
-                        u[:, g * P : (g + 1) * P],
+                        bank[:, first - part.start : first - part.start + P],
+                        u[:, first : first + P],
                         identity[:],
                         is_transpose=True,
-                        start=(t == 0 and place == 0),
-                        stop=(t == T - 1 and place == PER_BANK - 1),
+                        start=(t == 0 and first == part.start),
+                        stop=(t == T - 1 and first + P == part.stop),
                     )
-                if t == T - 1:
-                    for n in range(nodes.start // BANK, nodes.stop // BANK):
-                        finish_chunk(b, n)
 
-        def finish_chunk(b, n):
+        def finish(b, part, sum_bank):
+            width = part.stop - part.start
             flipped_sum = flipped_sums.tile([P, BANK], F32, name="flipped_sum")
-            for place in range(PER_BANK):
+            for first in range(0, width, P):
                 for h in range(HEADS):
-                    m = h * NODE_BLOCKS + n * PER_BANK + place
-                    head = slice(place * P + h * HALF, place * P + (h + 1) * HALF)
+                    m = h * NODE_BLOCKS + (part.start + first) // P
+                    head = slice(first + h * HALF, first + (h + 1) * HALF)
                     nc.scalar.activation(
-                        flipped_sum[:, head], sums[b][n][:, head], FUNC.Copy, scale=inverses[b][:, m : m + 1]
+                        flipped_sum[:, head], sum_bank[:, head], FUNC.Copy, scale=inverses[b][:, m : m + 1]
                     )
-            bank = banks.tile([P, BANK], F32, tag="bank")
-            project_into_bank(bank, w1_sb, b * P, n, False)
-            for place in range(PER_BANK):
+            bank = banks[1].tile([P, BANK], F32, tag="bank")
+            project_into_bank(bank, w1_sb, b * P, part, False)
+            for first in range(0, width, P):
                 nc.tensor.matmul(
-                    bank[:, place * P : (place + 1) * P],
-                    flipped_sum[:, place * P : (place + 1) * P],
+                    bank[:, first : first + P],
+                    flipped_sum[:, first : first + P],
                     identity[:],
                     is_transpose=True,
                     start=False,
-                    stop=(place == PER_BANK - 1),
+                    stop=(first + P == width),
                 )
             result = results.tile([P, BANK], F32, name="result")
-            nc.scalar.activation(result[:], bank[:], FUNC.Gelu, bias=bias_of(B1, b))
-            nc.scalar.dma_start(out[b * P : (b + 1) * P, n * BANK : (n + 1) * BANK], result[:])
+            nc.scalar.activation(result[:, 0:width], bank[:, 0:width], FUNC.Gelu, bias=bias_of(B1, b))
+            nc.scalar.dma_start(out[b * P : (b + 1) * P, part], result[:, 0:width])
 
-        tiles_in_order = [(kind, b) for b in range(BLOCKS) for kind in ("keys", "queries")]
-        tiles_in_order += [("values", b) for b in range(BLOCKS)]
-        chunks_in_order = [(kind, b, n) for kind, b in tiles_in_order for n in range(CHUNKS)]
-        at_once = 2 * CHUNKS
-        for kind, b, n in chunks_in_order[:at_once]:
-            project_chunk(kind, b, n)
-        for r in range(2 * BLOCKS):
+        def cut(start, stop, width):
+            return [slice(first, first + width) for first in range(start, stop, width)]
+
+        chunks = cut(0, S, BANK)
+        first_halves, last_halves = cut(0, BANK, HALF_BANK), cut(S - BANK, S, HALF_BANK)
+
+        def project_all(tiles, ring):
+            for kind, b in tiles:
+                for nodes in chunks:
+                    project(kind, b, nodes, ring)
+
+        def softmax_stages(r, t):
+            if 1 <= r <= BLOCKS and t == 1:
+                softmax_numerators(r - 1)
+            if 2 <= r <= BLOCKS + 1 and t == 0:
+                softmax_inverses(r - 2)
+
+        def key_round(b, first_runs):
+            after = [("keys", b + 1), ("queries", b + 1)] if b + 1 < BLOCKS else [("values", 0)]
+            project_all(after, 0)
             for t in range(T):
-                if r < BLOCKS:
-                    first = at_once + PER_PIECE * (r * T + t)
-                    for kind, b, n in chunks_in_order[first : first + PER_PIECE]:
-                        project_chunk(kind, b, n)
-                    key_piece(r, t, BANK if (r, t) == (0, 0) else S)
-                else:
-                    value_piece(r - BLOCKS, t, BANK if (r, t) == (2 * BLOCKS - 1, T - 1) else S)
-                if 2 <= r <= BLOCKS + 1 and t == 2:
-                    softmax_inverses(r - 2)
-                if 1 <= r <= BLOCKS and t == 2:
-                    softmax_numerators(r - 1)
+                key_piece(b, t, first_runs if t == 0 else [slice(0, S)])
+                softmax_stages(b, t)
+
+        def value_round(b, runs):
+            after = [("values", b + 1)] if b + 1 < BLOCKS else []
+            project_all(after, 1)
+            spreads = spread_numerators(b)
+            for run in runs:
+                parts = cut(run.start, run.stop, min(BANK, run.stop - run.start))
+                sums = [banks[0].tile([P, BANK], F32, tag="bank", name="sum_bank") for part in parts]
+                for t in range(T):
+                    value_look_up(b, t, run, spreads[t], parts, sums)
+                    softmax_stages(BLOCKS + b, t)
+                for part, bank in zip(parts, sums):
+                    finish(b, part, bank)
+
+        round_0 = [("keys", 0, nodes) for nodes in chunks[:-1]]
+        round_0 += [("queries", 0, first_halves[0])]
+        round_0 += [("keys", 0, nodes) for nodes in last_halves]
+        round_0 += [("queries", 0, nodes) for nodes in first_halves[1:] + chunks[1:]]
+        for kind, b, nodes in round_0:
+            project(kind, b, nodes, 0)
+
+        key_round(0, first_halves + chunks[1:])
+        key_round(1, [slice(0, S)])
+        key_round(2, [slice(0, S)])
+        key_round(3, [slice(0, S)])
+        value_round(0, [slice(0, S)])
+        value_round(1, [slice(0, S)])
+        value_round(2, [slice(0, S)])
+        value_round(3, [slice(0, 1024), slice(1024, 1536), slice(1536, 1792), slice(1792, 2048)])

@@ -203,7 +203,7 @@ def tile_attnno_b_kernel(tc, x, w0, b0, qw, qb, wkv, w1, b1, offs, out):
             numerators[b] = small.tile([P, P], F32, name="numerator")
             below = add_up([(identity, up_1), (identity, up_2)])
             nc.scalar.activation(numerators[b][:], below[:], FUNC.Exp, scale=-1.0)
-            nc.scalar.dma_start(
+            nc.sync.dma_start(
                 out[b * P : b * P + T * HEADS, :].rearrange("r (g s) -> (r g) s", s=P), numerators[b][:]
             )
 
@@ -277,9 +277,7 @@ def tile_attnno_b_kernel(tc, x, w0, b0, qw, qb, wkv, w1, b1, offs, out):
                     project(kind, b, nodes, ring)
 
         def softmax_stages(r, t):
-            if 1 <= r <= BLOCKS and t == 1:
-                softmax_numerators(r - 1)
-            if 2 <= r <= BLOCKS + 1 and t == 0:
+            if 2 <= r <= BLOCKS + 1 and t == 1:
                 softmax_inverses(r - 2)
 
         def key_round(b, first_runs):
@@ -288,6 +286,7 @@ def tile_attnno_b_kernel(tc, x, w0, b0, qw, qb, wkv, w1, b1, offs, out):
             for t in range(T):
                 key_piece(b, t, first_runs if t == 0 else [slice(0, S)])
                 softmax_stages(b, t)
+            softmax_numerators(b)
 
         def value_round(b, runs):
             after = [("values", b + 1)] if b + 1 < BLOCKS else []

@@ -203,7 +203,7 @@ def tile_attnno_b_kernel(tc, x, w0, b0, qw, qb, wkv, w1, b1, offs, out):
             numerators[b] = small.tile([P, P], F32, name="numerator")
             below = add_up([(identity, up_1), (identity, up_2)])
             nc.scalar.activation(numerators[b][:], below[:], FUNC.Exp, scale=-1.0)
-            nc.sync.dma_start(
+            nc.scalar.dma_start(
                 out[b * P : b * P + T * HEADS, :].rearrange("r (g s) -> (r g) s", s=P), numerators[b][:]
             )
 

@@ -163,27 +163,24 @@ def tile_attnno_b_kernel(tc, x, w0, b0, qw, qb, wkv, w1, b1, offs, out):
 
         scores = {}
 
-        def key_piece(b, t, runs):
-            if t == 0:
-                scores[b] = banks[1].tile([P, P], F32, tag="bank", name="scores")
+        def key_look_up(b, t, nodes):
             e = products.tile([P, S], F32, name="product")
+            nc.vector.tensor_tensor(
+                e[:, nodes],
+                projected["keys", b][:].indirect(list_of(t, nodes)),
+                projected["queries", b][:, nodes],
+                ALU.mult,
+            )
             e_bf = rounded.tile([P, S], BF16, name="e_bf")
-            for nodes in runs:
-                nc.vector.tensor_tensor(
-                    e[:, nodes],
-                    projected["keys", b][:].indirect(list_of(t, nodes)),
-                    projected["queries", b][:, nodes],
-                    ALU.mult,
+            nc.scalar.copy(e_bf[:, nodes], e[:, nodes])
+            for g in range(nodes.start // P, nodes.stop // P):
+                nc.tensor.matmul(
+                    scores[b][:],
+                    head_sum_of(t, g),
+                    e_bf[:, g * P : (g + 1) * P],
+                    start=(t == 0 and g == 0),
+                    stop=(t == T - 1 and g == NODE_BLOCKS - 1),
                 )
-                nc.scalar.copy(e_bf[:, nodes], e[:, nodes])
-                for g in range(nodes.start // P, nodes.stop // P):
-                    nc.tensor.matmul(
-                        scores[b][:],
-                        head_sum_of(t, g),
-                        e_bf[:, g * P : (g + 1) * P],
-                        start=(t == 0 and g == 0),
-                        stop=(t == T - 1 and g == NODE_BLOCKS - 1),
-                    )
 
         numerators = {}
 
@@ -269,7 +266,6 @@ def tile_attnno_b_kernel(tc, x, w0, b0, qw, qb, wkv, w1, b1, offs, out):
             return [slice(first, first + width) for first in range(start, stop, width)]
 
         chunks = cut(0, S, BANK)
-        first_halves, last_halves = cut(0, BANK, HALF_BANK), cut(S - BANK, S, HALF_BANK)
 
         def project_all(tiles, ring):
             for kind, b in tiles:
@@ -280,12 +276,14 @@ def tile_attnno_b_kernel(tc, x, w0, b0, qw, qb, wkv, w1, b1, offs, out):
             if 2 <= r <= BLOCKS + 1 and t == 1:
                 softmax_inverses(r - 2)
 
-        def key_round(b, first_runs):
+        def key_round(b, runs):
             after = [("keys", b + 1), ("queries", b + 1)] if b + 1 < BLOCKS else [("values", 0)]
             project_all(after, 0)
-            for t in range(T):
-                key_piece(b, t, first_runs if t == 0 else [slice(0, S)])
-                softmax_stages(b, t)
+            scores[b] = banks[1].tile([P, P], F32, tag="bank", name="scores")
+            for run in runs:
+                for t in range(T):
+                    key_look_up(b, t, run)
+                    softmax_stages(b, t)
             softmax_numerators(b)
 
         def value_round(b, runs):
@@ -302,13 +300,13 @@ def tile_attnno_b_kernel(tc, x, w0, b0, qw, qb, wkv, w1, b1, offs, out):
                     finish(b, part, bank)
 
         round_0 = [("keys", 0, nodes) for nodes in chunks[:-1]]
-        round_0 += [("queries", 0, first_halves[0])]
-        round_0 += [("keys", 0, nodes) for nodes in last_halves]
-        round_0 += [("queries", 0, nodes) for nodes in first_halves[1:] + chunks[1:]]
+        round_0 += [("queries", 0, chunks[0])]
+        round_0 += [("keys", 0, nodes) for nodes in cut(S - BANK, S, HALF_BANK)]
+        round_0 += [("queries", 0, nodes) for nodes in chunks[1:]]
         for kind, b, nodes in round_0:
             project(kind, b, nodes, 0)
 
-        key_round(0, first_halves + chunks[1:])
+        key_round(0, [slice(0, BANK), slice(BANK, S)])
         key_round(1, [slice(0, S)])
         key_round(2, [slice(0, S)])
         key_round(3, [slice(0, S)])

@@ -172,15 +172,16 @@ def tile_attnno_b_kernel(tc, x, w0, b0, qw, qb, wkv, w1, b1, offs, out):
                 ALU.mult,
             )
             e_bf = rounded.tile([P, S], BF16, name="e_bf")
-            nc.scalar.copy(e_bf[:, nodes], e[:, nodes])
-            for g in range(nodes.start // P, nodes.stop // P):
-                nc.tensor.matmul(
-                    scores[b][:],
-                    head_sum_of(t, g),
-                    e_bf[:, g * P : (g + 1) * P],
-                    start=(t == 0 and g == 0),
-                    stop=(t == T - 1 and g == NODE_BLOCKS - 1),
-                )
+            for part in cut(nodes.start, nodes.stop, BANK):
+                nc.scalar.copy(e_bf[:, part], e[:, part])
+                for g in range(part.start // P, part.stop // P):
+                    nc.tensor.matmul(
+                        scores[b][:],
+                        head_sum_of(t, g),
+                        e_bf[:, g * P : (g + 1) * P],
+                        start=(t == 0 and g == 0),
+                        stop=(t == T - 1 and g == NODE_BLOCKS - 1),
+                    )
 
         numerators = {}
 
@@ -313,4 +314,4 @@ def tile_attnno_b_kernel(tc, x, w0, b0, qw, qb, wkv, w1, b1, offs, out):
         value_round(0, [slice(0, S)])
         value_round(1, [slice(0, S)])
         value_round(2, [slice(0, S)])
-        value_round(3, [slice(0, 1024), slice(1024, 1536), slice(1536, 1792), slice(1792, 2048)])
+        value_round(3, [slice(0, 1024), slice(1024, 1536), slice(1536, 1920), slice(1920, 2048)])

@@ -42,7 +42,7 @@ def tile_attnno_b_kernel(tc, x, w0, b0, qw, qb, wkv, w1, b1, offs, out):
         queries = ctx.enter_context(tc.tile_pool(name="queries", bufs=3))
         products = ctx.enter_context(tc.tile_pool(name="products", bufs=6))
         rounded = ctx.enter_context(tc.tile_pool(name="rounded", bufs=2))
-        results = ctx.enter_context(tc.tile_pool(name="results", bufs=CHUNKS))
+        results = ctx.enter_context(tc.tile_pool(name="results", bufs=3))
         flipped_sums = ctx.enter_context(tc.tile_pool(name="flipped_sums", bufs=2))
         small = ctx.enter_context(tc.tile_pool(name="small", bufs=2))
         kept = ctx.enter_context(tc.tile_pool(name="kept", bufs=BLOCKS))
@@ -198,20 +198,24 @@ def tile_attnno_b_kernel(tc, x, w0, b0, qw, qb, wkv, w1, b1, offs, out):
             nc.scalar.activation(up_1[:], add_up([(over_1, score)])[:], FUNC.Relu)
             up_2 = small.tile([P, P], F32, name="up_2")
             nc.scalar.activation(up_2[:], add_up([(over_2, score), (over_2, up_1)])[:], FUNC.Relu)
-            numerators[b] = small.tile([P, P], F32, name="numerator")
+            numerators[b] = kept.tile([P, P], F32, name="numerator")
             below = add_up([(identity, up_1), (identity, up_2)])
             nc.scalar.activation(numerators[b][:], below[:], FUNC.Exp, scale=-1.0)
             nc.scalar.dma_start(
                 out[b * P : b * P + T * HEADS, :].rearrange("r (g s) -> (r g) s", s=P), numerators[b][:]
             )
 
-        inverses = {}
-
-        def softmax_inverses(b):
-            summed = banks[1].tile([P, GROUPS], F32, tag="bank", name="summed")
-            nc.tensor.matmul(summed[:], numerators[b][:], same_m[:], start=True, stop=True)
-            inverses[b] = kept.tile([P, GROUPS], F32, name="inverse")
-            nc.vector.reciprocal(inverses[b][:], summed[:])
+        def softmax_inverses():
+            summed = banks[1].tile([P, BLOCKS * GROUPS], F32, tag="bank", name="summed")
+            for b in range(BLOCKS):
+                nc.tensor.matmul(
+                    summed[:, b * GROUPS : (b + 1) * GROUPS], numerators[b][:], same_m[:], start=True, stop=True
+                )
+            log_sum = small.tile([P, BLOCKS * GROUPS], F32, name="log_sum")
+            nc.scalar.activation(log_sum[:], summed[:], FUNC.Ln)
+            inverses = held.tile([P, BLOCKS * GROUPS], F32, name="inverses")
+            nc.scalar.activation(inverses[:], log_sum[:], FUNC.Exp, scale=-1.0)
+            return inverses
 
         def spread_numerators(b):
             spreads = [streamed.tile([P, S], F32, name="spread", tag="streamed") for t in range(T)]
@@ -243,10 +247,10 @@ def tile_attnno_b_kernel(tc, x, w0, b0, qw, qb, wkv, w1, b1, offs, out):
             flipped_sum = flipped_sums.tile([P, BANK], F32, name="flipped_sum")
             for first in range(0, width, P):
                 for h in range(HEADS):
-                    m = h * NODE_BLOCKS + (part.start + first) // P
+                    m = b * GROUPS + h * NODE_BLOCKS + (part.start + first) // P
                     head = slice(first + h * HALF, first + (h + 1) * HALF)
                     nc.scalar.activation(
-                        flipped_sum[:, head], sum_bank[:, head], FUNC.Copy, scale=inverses[b][:, m : m + 1]
+                        flipped_sum[:, head], sum_bank[:, head], FUNC.Copy, scale=inverses[:, m : m + 1]
                     )
             bank = banks[1].tile([P, BANK], F32, tag="bank")
             project_into_bank(bank, w1_sb, b * P, part, False)
@@ -273,30 +277,20 @@ def tile_attnno_b_kernel(tc, x, w0, b0, qw, qb, wkv, w1, b1, offs, out):
                 for nodes in chunks:
                     project(kind, b, nodes, ring)
 
-        def softmax_stages(r, t):
-            if 2 <= r <= BLOCKS + 1 and t == 1:
-                softmax_inverses(r - 2)
-
         def key_round(b, runs):
-            after = [("keys", b + 1), ("queries", b + 1)] if b + 1 < BLOCKS else [("values", 0)]
-            project_all(after, 0)
             scores[b] = banks[1].tile([P, P], F32, tag="bank", name="scores")
             for run in runs:
                 for t in range(T):
                     key_look_up(b, t, run)
-                    softmax_stages(b, t)
             softmax_numerators(b)
 
         def value_round(b, runs):
-            after = [("values", b + 1)] if b + 1 < BLOCKS else []
-            project_all(after, 1)
             spreads = spread_numerators(b)
             for run in runs:
                 parts = cut(run.start, run.stop, min(BANK, run.stop - run.start))
                 sums = [banks[0].tile([P, BANK], F32, tag="bank", name="sum_bank") for part in parts]
                 for t in range(T):
                     value_look_up(b, t, run, spreads[t], parts, sums)
-                    softmax_stages(BLOCKS + b, t)
                 for part, bank in zip(parts, sums):
                     finish(b, part, bank)
 
@@ -307,11 +301,19 @@ def tile_attnno_b_kernel(tc, x, w0, b0, qw, qb, wkv, w1, b1, offs, out):
         for kind, b, nodes in round_0:
             project(kind, b, nodes, 0)
 
+        project_all([("keys", 1), ("queries", 1)], 0)
         key_round(0, [slice(0, BANK), slice(BANK, S)])
+        project_all([("keys", 2), ("queries", 2)], 0)
         key_round(1, [slice(0, S)])
+        project_all([("keys", 3), ("queries", 3)], 0)
         key_round(2, [slice(0, S)])
+        project_all([("values", 0)], 0)
         key_round(3, [slice(0, S)])
+        project_all([("values", 1)], 1)
+        inverses = softmax_inverses()
         value_round(0, [slice(0, S)])
+        project_all([("values", 2)], 1)
         value_round(1, [slice(0, S)])
+        project_all([("values", 3)], 1)
         value_round(2, [slice(0, S)])
         value_round(3, [slice(0, 1024), slice(1024, 1536), slice(1536, 1920), slice(1920, 2048)])

@@ -205,17 +205,27 @@ def tile_attnno_b_kernel(tc, x, w0, b0, qw, qb, wkv, w1, b1, offs, out):
                 out[b * P : b * P + T * HEADS, :].rearrange("r (g s) -> (r g) s", s=P), numerators[b][:]
             )
 
-        def softmax_inverses():
+        inverses = held.tile([P, BLOCKS * GROUPS], F32, name="inverses")
+
+        def sums_of_numerators(blocks):
             summed = banks[1].tile([P, BLOCKS * GROUPS], F32, tag="bank", name="summed")
-            for b in range(BLOCKS):
+            for b in blocks:
                 nc.tensor.matmul(
                     summed[:, b * GROUPS : (b + 1) * GROUPS], numerators[b][:], same_m[:], start=True, stop=True
                 )
+            return summed
+
+        def first_inverses():
+            columns = slice(0, (BLOCKS - 1) * GROUPS)
+            summed = sums_of_numerators(range(BLOCKS - 1))
             log_sum = small.tile([P, BLOCKS * GROUPS], F32, name="log_sum")
-            nc.scalar.activation(log_sum[:], summed[:], FUNC.Ln)
-            inverses = held.tile([P, BLOCKS * GROUPS], F32, name="inverses")
-            nc.scalar.activation(inverses[:], log_sum[:], FUNC.Exp, scale=-1.0)
-            return inverses
+            nc.scalar.activation(log_sum[:, columns], summed[:, columns], FUNC.Ln)
+            nc.scalar.activation(inverses[:, columns], log_sum[:, columns], FUNC.Exp, scale=-1.0)
+
+        def last_inverses():
+            columns = slice((BLOCKS - 1) * GROUPS, BLOCKS * GROUPS)
+            summed = sums_of_numerators([BLOCKS - 1])
+            nc.vector.reciprocal(inverses[:, columns], summed[:, columns])
 
         def spread_numerators(b):
             spreads = [streamed.tile([P, S], F32, name="spread", tag="streamed") for t in range(T)]
@@ -291,6 +301,8 @@ def tile_attnno_b_kernel(tc, x, w0, b0, qw, qb, wkv, w1, b1, offs, out):
                 sums = [banks[0].tile([P, BANK], F32, tag="bank", name="sum_bank") for part in parts]
                 for t in range(T):
                     value_look_up(b, t, run, spreads[t], parts, sums)
+                    if (b, t) == (1, 1):
+                        last_inverses()
                 for part, bank in zip(parts, sums):
                     finish(b, part, bank)
 
@@ -308,9 +320,9 @@ def tile_attnno_b_kernel(tc, x, w0, b0, qw, qb, wkv, w1, b1, offs, out):
         project_all([("keys", 3), ("queries", 3)], 0)
         key_round(2, [slice(0, S)])
         project_all([("values", 0)], 0)
+        first_inverses()
         key_round(3, [slice(0, S)])
         project_all([("values", 1)], 1)
-        inverses = softmax_inverses()
         value_round(0, [slice(0, S)])
         project_all([("values", 2)], 1)
         value_round(1, [slice(0, S)])

@@ -230,10 +230,12 @@ def tile_attnno_b_kernel(tc, x, w0, b0, qw, qb, wkv, w1, b1, offs, out):
         def spread_numerators(b):
             spreads = [streamed.tile([P, S], F32, name="spread", tag="streamed") for t in range(T)]
             for t in range(T):
-                for h in range(HEADS):
-                    nc.sync.dma_start(
-                        spreads[t][h * HALF : (h + 1) * HALF, :], out[b * P + t * HEADS + h, :].partition_broadcast(HALF)
-                    )
+                for nodes in cut(0, S, S // 2):
+                    for h in range(HEADS):
+                        nc.sync.dma_start(
+                            spreads[t][h * HALF : (h + 1) * HALF, nodes],
+                            out[b * P + t * HEADS + h, nodes].partition_broadcast(HALF),
+                        )
             return spreads
 
         def value_look_up(b, t, nodes, spread, parts, sums):

from contextlib import ExitStack

import concourse.mybir as mybir
from concourse.masks import make_identity

F32 = mybir.dt.float32
BF16 = mybir.dt.bfloat16
U16 = mybir.dt.uint16
FUNC = mybir.ActivationFunctionType
ALU = mybir.AluOpType
AXIS = mybir.AxisListType

P = 128
C = 512
S = 2048
T = 4
BLOCKS = C // P
HEADS = 2
HALF = P // HEADS
BANK = 512
HALF_BANK = BANK // 2
PSUM_BANKS = 8
CHUNKS = S // BANK
NODE_BLOCKS = S // P
GROUPS = HEADS * NODE_BLOCKS
LIST_COLS = S // 16
B0, QB, B1 = 0, 1, 2

PER_BANK = BANK // P
STREAMED = 9

FLOPS = 2 * C * S * 5 * C + 2 * C * T * S


def tile_attnno_b_kernel(tc, x, w0, b0, qw, qb, wkv, w1, b1, offs, out):
    nc = tc.nc
    with ExitStack() as ctx:
        held = ctx.enter_context(tc.tile_pool(name="held", bufs=1))
        streamed = ctx.enter_context(tc.tile_pool(name="streamed", bufs=STREAMED))
        staged = ctx.enter_context(tc.tile_pool(name="staged", bufs=2))
        windows = ctx.enter_context(tc.tile_pool(name="windows", bufs=3))
        queries = ctx.enter_context(tc.tile_pool(name="queries", bufs=3))
        products = ctx.enter_context(tc.tile_pool(name="products", bufs=6))
        rounded = ctx.enter_context(tc.tile_pool(name="rounded", bufs=2))
        results = ctx.enter_context(tc.tile_pool(name="results", bufs=3))
        flipped_sums = ctx.enter_context(tc.tile_pool(name="flipped_sums", bufs=2))
        small = ctx.enter_context(tc.tile_pool(name="small", bufs=2))
        kept = ctx.enter_context(tc.tile_pool(name="kept", bufs=BLOCKS))
        banks = [ctx.enter_context(tc.psum_pool(name=f"banks_{i}", bufs=PSUM_BANKS // 2)) for i in range(2)]

        def load_weight(w, name):
            w_sb = held.tile([P, BLOCKS, w.shape[1]], BF16, name=name)
            nc.sync.dma_start(w_sb[:], w.rearrange("(k p) c -> p k c", p=P))
            return w_sb

        biases = [held.tile([P, BLOCKS], F32, name=f"bias_{which}") for which in (B0, QB, B1)]

        def load_biases():
            for which, vec in enumerate((b0, qb, b1)):
                nc.scalar.dma_start(biases[which][:], vec.rearrange("(b p) o -> p (b o)", p=P))

        def bias_of(which, b):
            return biases[which][:, b : b + 1]

        identity = held.tile([P, P], F32, name="identity")
        make_identity(nc, identity[:])

        w0_sb = held.tile([P, BLOCKS, C], BF16, name="w0_sb")
        x1 = [held.tile([P, BLOCKS, BANK], BF16, name=f"x1_{n}") for n in range(CHUNKS)]
        for n in range(CHUNKS):
            x_f32 = streamed.tile([P, BLOCKS, BANK], F32, name="x_f32", tag="streamed")
            x_bf = staged.tile([P, BLOCKS, BANK], BF16, name="x_bf")
            x1_banks = [banks[n % 2].tile([P, BANK], F32, tag="bank", name="x1_bank") for b in range(BLOCKS)]
            for k in range(BLOCKS):
                if n == 0:
                    nc.scalar.dma_start(w0_sb[:, k, :], w0[k * P : (k + 1) * P, :])
                width = HALF_BANK if n == 0 and k == 0 else BANK
                for first in range(0, BANK, width):
                    cols = slice(first, first + width)
                    nc.sync.dma_start(
                        x_f32[:, k, cols], x[k * P : (k + 1) * P, n * BANK + first : n * BANK + first + width]
                    )
                    nc.vector.tensor_copy(x_bf[:, k, cols], x_f32[:, k, cols])
                    for b in range(BLOCKS):
                        nc.tensor.matmul(
                            x1_banks[b][:, cols],
                            w0_sb[:, k, b * P : (b + 1) * P],
                            x_bf[:, k, cols],
                            start=(k == 0 and first == 0),
                            stop=(k == BLOCKS - 1),
                        )
            if n == 0:
                load_biases()
            for b in range(BLOCKS):
                nc.scalar.activation(x1[n][:, b, :], x1_banks[b][:], FUNC.Gelu, bias=bias_of(B0, b))

        last_row = P - NODE_BLOCKS - 1
        strip = held.tile([P, last_row + P], BF16, name="strip")
        nc.vector.memset(strip[:], 0.0)
        for h in range(HEADS):
            column = last_row + h * NODE_BLOCKS
            nc.vector.memset(strip[h * HALF : (h + 1) * HALF, column : column + 1], 0.125)

        def head_sum_of(t, g):
            start = last_row - (t * GROUPS + g)
            return strip[:, start : start + P]

        def rows_of(t):
            return slice(t * GROUPS, (t + 1) * GROUPS)

        over_1 = held.tile([P, P], F32, name="over_1")
        over_2 = held.tile([P, P], F32, name="over_2")
        for t in range(T):
            own = identity[:, rows_of(t)]
            nc.vector.tensor_tensor(over_1[:, rows_of(t)], identity[:, rows_of(t ^ 1)], own, ALU.subtract)
            nc.vector.tensor_tensor(over_2[:, rows_of(t)], identity[:, rows_of(t ^ 2)], own, ALU.subtract)
        same_m = held.tile([P, GROUPS], F32, name="same_m")
        nc.vector.tensor_reduce(same_m[:], identity[:].rearrange("p (t m) -> p m t", t=T), AXIS.X, ALU.add)

        wkv_sb = load_weight(wkv, "wkv_sb")
        qw_sb = load_weight(qw, "qw_sb")
        offsets = held.tile([P, T * LIST_COLS], U16, name="offsets")
        nc.sync.dma_start(offsets[:], offs)
        w1_sb = load_weight(w1, "w1_sb")

        def project_into_bank(bank, w_sb, first_col, nodes, stop):
            n, place = divmod(nodes.start, BANK)
            width = nodes.stop - nodes.start
            for k in range(BLOCKS):
                nc.tensor.matmul(
                    bank[:, 0:width],
                    w_sb[:, k, first_col : first_col + P],
                    x1[n][:, k, place : place + width],
                    start=(k == 0),
                    stop=(stop and k == BLOCKS - 1),
                )

        projected = {}

        def project(kind, b, nodes, ring):
            if nodes.start == 0 and kind == "queries":
                projected[kind, b] = queries.tile([P, S], F32, name="q")
            elif nodes.start == 0:
                projected[kind, b] = windows.tile([P, S], F32, name="window")
            chunk = projected[kind, b][:, nodes]
            bank = banks[ring].tile([P, BANK], F32, tag="bank")
            made = bank[:, 0 : nodes.stop - nodes.start]
            if kind == "keys" and b == 0:
                project_into_bank(bank, wkv_sb, b * P, nodes, True)
                nc.vector.tensor_copy(chunk, made)
            elif kind == "keys":
                project_into_bank(bank, wkv_sb, b * P, nodes, True)
                nc.scalar.copy(chunk, made)
            elif kind == "values":
                project_into_bank(bank, wkv_sb, C + b * P, nodes, True)
                nc.scalar.copy(chunk, made)
            else:
                project_into_bank(bank, qw_sb, b * P, nodes, True)
                nc.scalar.activation(chunk, made, FUNC.Identity, bias=bias_of(QB, b))

        def list_of(t, nodes):
            return offsets[:, (t * S + nodes.start) // 16 : (t * S + nodes.stop) // 16]

        scores = {}

        def key_look_up(b, t, nodes):
            e = products.tile([P, S], F32, name="product")
            nc.vector.tensor_tensor(
                e[:, nodes],
                projected["keys", b][:].indirect(list_of(t, nodes)),
                projected["queries", b][:, nodes],
                ALU.mult,
            )
            e_bf = rounded.tile([P, S], BF16, name="e_bf")
            for part in cut(nodes.start, nodes.stop, BANK):
                nc.scalar.copy(e_bf[:, part], e[:, part])
                for g in range(part.start // P, part.stop // P):
                    nc.tensor.matmul(
                        scores[b][:],
                        head_sum_of(t, g),
                        e_bf[:, g * P : (g + 1) * P],
                        start=(t == 0 and g == 0),
                        stop=(t == T - 1 and g == NODE_BLOCKS - 1),
                    )

        numerators = {}

        def add_up(terms):
            total = banks[1].tile([P, P], F32, tag="bank", name="total")
            for i, (stationary, moving) in enumerate(terms):
                nc.tensor.matmul(total[:], stationary[:], moving[:], start=(i == 0), stop=(i == len(terms) - 1))
            return total

        def softmax_numerators(b):
            score = small.tile([P, P], F32, name="score")
            nc.scalar.copy(score[:], scores[b][:])
            up_1 = small.tile([P, P], F32, name="up_1")
            nc.scalar.activation(up_1[:], add_up([(over_1, score)])[:], FUNC.Relu)
            up_2 = small.tile([P, P], F32, name="up_2")
            nc.scalar.activation(up_2[:], add_up([(over_2, score), (over_2, up_1)])[:], FUNC.Relu)
            numerators[b] = kept.tile([P, P], F32, name="numerator")
            below = add_up([(identity, up_1), (identity, up_2)])
            nc.scalar.activation(numerators[b][:], below[:], FUNC.Exp, scale=-1.0)
            nc.scalar.dma_start(
                out[b * P : b * P + T * HEADS, :].rearrange("r (g s) -> (r g) s", s=P), numerators[b][:]
            )

        inverses = held.tile([P, BLOCKS * GROUPS], F32, name="inverses")

        def sums_of_numerators(blocks):
            summed = banks[1].tile([P, BLOCKS * GROUPS], F32, tag="bank", name="summed")
            for b in blocks:
                nc.tensor.matmul(
                    summed[:, b * GROUPS : (b + 1) * GROUPS], numerators[b][:], same_m[:], start=True, stop=True
                )
            return summed

        def first_inverses():
            columns = slice(0, (BLOCKS - 1) * GROUPS)
            summed = sums_of_numerators(range(BLOCKS - 1))
            log_sum = small.tile([P, BLOCKS * GROUPS], F32, name="log_sum")
            nc.scalar.activation(log_sum[:, columns], summed[:, columns], FUNC.Ln)
            nc.scalar.activation(inverses[:, columns], log_sum[:, columns], FUNC.Exp, scale=-1.0)

        def last_inverses():
            columns = slice((BLOCKS - 1) * GROUPS, BLOCKS * GROUPS)
            summed = sums_of_numerators([BLOCKS - 1])
            nc.vector.reciprocal(inverses[:, columns], summed[:, columns])

        def spread_numerators(b):
            spreads = [streamed.tile([P, S], F32, name="spread", tag="streamed") for t in range(T)]
            for t in range(T):
                for nodes in cut(0, S, S // 2):
                    for h in range(HEADS):
                        nc.sync.dma_start(
                            spreads[t][h * HALF : (h + 1) * HALF, nodes],
                            out[b * P + t * HEADS + h, nodes].partition_broadcast(HALF),
                        )
            return spreads

        def value_look_up(b, t, nodes, spread, parts, sums):
            u = products.tile([P, S], F32, name="product")
            nc.vector.tensor_tensor(
                u[:, nodes], projected["values", b][:].indirect(list_of(t, nodes)), spread[:, nodes], ALU.mult
            )
            for part, bank in zip(parts, sums):
                for first in range(part.start, part.stop, P):
                    nc.tensor.matmul(
                        bank[:, first - part.start : first - part.start + P],
                        u[:, first : first + P],
                        identity[:],
                        is_transpose=True,
                        start=(t == 0 and first == part.start),
                        stop=(t == T - 1 and first + P == part.stop),
                    )

        def finish(b, part, sum_bank):
            width = part.stop - part.start
            flipped_sum = flipped_sums.tile([P, BANK], F32, name="flipped_sum")
            for first in range(0, width, P):
                for h in range(HEADS):
                    m = b * GROUPS + h * NODE_BLOCKS + (part.start + first) // P
                    head = slice(first + h * HALF, first + (h + 1) * HALF)
                    nc.scalar.activation(
                        flipped_sum[:, head], sum_bank[:, head], FUNC.Copy, scale=inverses[:, m : m + 1]
                    )
            bank = banks[1].tile([P, BANK], F32, tag="bank")
            project_into_bank(bank, w1_sb, b * P, part, False)
            for first in range(0, width, P):
                nc.tensor.matmul(
                    bank[:, first : first + P],
                    flipped_sum[:, first : first + P],
                    identity[:],
                    is_transpose=True,
                    start=False,
                    stop=(first + P == width),
                )
            result = results.tile([P, BANK], F32, name="result")
            nc.scalar.activation(result[:, 0:width], bank[:, 0:width], FUNC.Gelu, bias=bias_of(B1, b))
            nc.scalar.dma_start(out[b * P : (b + 1) * P, part], result[:, 0:width])

        def cut(start, stop, width):
            return [slice(first, first + width) for first in range(start, stop, width)]

        chunks = cut(0, S, BANK)

        def project_all(tiles, ring):
            for kind, b in tiles:
                for nodes in chunks:
                    project(kind, b, nodes, ring)

        def key_round(b, runs):
            scores[b] = banks[1].tile([P, P], F32, tag="bank", name="scores")
            for run in runs:
                for t in range(T):
                    key_look_up(b, t, run)
            softmax_numerators(b)

        def value_round(b, runs):
            spreads = spread_numerators(b)
            for run in runs:
                parts = cut(run.start, run.stop, min(BANK, run.stop - run.start))
                sums = [banks[0].tile([P, BANK], F32, tag="bank", name="sum_bank") for part in parts]
                for t in range(T):
                    value_look_up(b, t, run, spreads[t], parts, sums)
                    if (b, t) == (1, 1):
                        last_inverses()
                for part, bank in zip(parts, sums):
                    finish(b, part, bank)

        round_0 = [("keys", 0, nodes) for nodes in chunks[:-1]]
        round_0 += [("queries", 0, chunks[0])]
        round_0 += [("keys", 0, nodes) for nodes in cut(S - BANK, S, HALF_BANK)]
        round_0 += [("queries", 0, nodes) for nodes in chunks[1:]]
        for kind, b, nodes in round_0:
            project(kind, b, nodes, 0)

        project_all([("keys", 1), ("queries", 1)], 0)
        key_round(0, [slice(0, BANK), slice(BANK, S)])
        project_all([("keys", 2), ("queries", 2)], 0)
        key_round(1, [slice(0, S)])
        project_all([("keys", 3), ("queries", 3)], 0)
        key_round(2, [slice(0, S)])
        project_all([("values", 0)], 0)
        first_inverses()
        key_round(3, [slice(0, S)])
        project_all([("values", 1)], 1)
        value_round(0, [slice(0, S)])
        project_all([("values", 2)], 1)
        value_round(1, [slice(0, S)])
        project_all([("values", 3)], 1)
        value_round(2, [slice(0, S)])
        value_round(3, [slice(0, 1024), slice(1024, 1536), slice(1536, 1920), slice(1920, 2048)])
